import numpy as np
import ml_dtypes


def mxq(x, axis, fmt="e4m3"):
    dtype, down = {"e4m3": (ml_dtypes.float8_e4m3fn, 7), "e5m2": (ml_dtypes.float8_e5m2, 14)}[fmt]
    v = np.moveaxis(np.asarray(x, np.float32).astype(ml_dtypes.bfloat16).astype(np.float64), axis, -1)
    blocks = v.reshape(v.shape[:-1] + (-1, 32))
    amax = np.abs(blocks).max(-1, keepdims=True)
    byte = np.maximum(np.where(amax > 0, np.frexp(amax)[1] - 1 + 127, 0) - down, 1)
    scale = np.exp2(byte - 127.0)
    codes = (blocks / scale).astype(np.float32).astype(dtype).astype(np.float64)
    return np.moveaxis((codes * scale).reshape(v.shape), -1, axis)


WIDE = False


def mx_kscale(k):
    if not WIDE:
        return np.ones(k)
    levels = np.array([10, -10, 5, -5, 0])
    a = np.random.permutation(np.resize(levels, k // 512 * 4)).reshape(k // 512, 4)
    idx = np.arange(k)
    return np.exp2(a[idx // 512, idx % 128 // 32])


BF16 = ml_dtypes.bfloat16


def bf(x):
    return np.asarray(x, np.float32).astype(BF16)


def f64(x):
    return np.asarray(x).astype(np.float64)


B, C, P, D = 16, 512, 128, 512
EPS = 1e-5


def layer_norm(v, w, b):
    m = v.mean(-1, keepdims=True)
    var = ((v - m) ** 2).mean(-1, keepdims=True)
    return (v - m) * (1.0 / np.sqrt(var + EPS)) * w + b


def setup_inputs():
    s = mx_kscale(2 * D)
    return {"prev_cell_out": bf(np.random.standard_normal((B, P, D)) * s[D:]),
            "emb_prompt": bf(np.random.standard_normal((P, D)) / np.sqrt(D)),
            "ln_prompt_w": bf((1.0 + 0.1 * np.random.standard_normal(D)) * s[:D]),
            "ln_prompt_b": bf(0.1 * np.random.standard_normal(D) * s[:D]),
            "W_imp": bf(np.random.standard_normal((2 * D, D)) / D / s[:, None]),
            "b_imp": bf(np.random.standard_normal(D) / np.sqrt(D)),
            "emb_column": bf(0.01 * np.random.standard_normal((C, D))),
            "ln_col_w": bf(1.0 + 0.1 * np.random.standard_normal(D)),
            "ln_col_b": bf(0.1 * np.random.standard_normal(D))}


def reference(prev_cell_out, emb_prompt, ln_prompt_w, ln_prompt_b, W_imp, b_imp, emb_column, ln_col_w, ln_col_b):
    p0 = f64(emb_prompt)
    w = f64(W_imp)
    pn = layer_norm(p0, f64(ln_prompt_w), f64(ln_prompt_b))
    from_prompt = mxq(pn, 1, "e4m3") @ mxq(w[:D], 0, "e4m3")
    from_prev = mxq(f64(prev_cell_out), 2, "e4m3") @ mxq(w[D:], 0, "e4m3")
    x_prompt = from_prompt[None] + from_prev + f64(b_imp) + p0[None]
    col_t = layer_norm(f64(emb_column), f64(ln_col_w), f64(ln_col_b)).T
    return mxq(x_prompt, 2, "e4m3") @ mxq(col_t, 0, "e4m3")

@@ -1,0 +1,414 @@
+from contextlib import ExitStack
+
+import concourse.mybir as mybir
+from concourse.masks import make_identity
+
+F32 = mybir.dt.float32
+BF16 = mybir.dt.bfloat16
+U32 = mybir.dt.uint32
+U8 = mybir.dt.uint8
+FP8X4 = mybir.dt.float8_e4m3fn_x4
+ALU = mybir.AluOpType
+ACT = mybir.ActivationFunctionType
+
+P = 128
+D = 512
+B = 16
+T = 4
+EPS = 1e-5
+CH = 2
+NCH = B // CH
+WP1 = 4
+WP2 = 4
+CPARTS = 2
+
+FLOPS = 2 * P * D * D + 2 * 2 * B * P * D * D
+
+ENG = {
+    "p0b": "S",
+    "wrg1_3": "S",
+    "wrg1_1": "S",
+    "wrg1_2": "S",
+    "pnact": "S",
+    "wrg2_3": "S",
+    "CP0": "S",
+    "wrg2_0": "S",
+    "CP2": "S",
+    "CP1": "S",
+    "zc3": "S",
+    "CP4": "S",
+    "zc0": "S",
+    "CP3": "S",
+    "cact2": "S",
+    "cact1": "S",
+    "cact3": "S",
+    "crg1": "S",
+    "CP6": "S",
+    "CP5": "S",
+    "CP7": "S",
+    "CO1": "S",
+    "CO0": "S",
+    "CO2": "S",
+    "CO3": "S",
+    "CO5": "S",
+    "CO4": "S",
+    "CO6": "S",
+    "CO7": "S",
+    "CO9": "S",
+    "CO8": "S",
+    "CO10": "S",
+    "CO11": "S",
+    "CO13": "S",
+    "CO15": "S",
+    "wrg1_0": "G",
+    "wrg2_1": "G",
+    "wrg2_2": "G",
+    "zc2": "G",
+    "zc1": "G",
+    "crg0": "G",
+}
+
+ORDER = (
+    "idf", "ms", "warm", "vec", "idb", "p0", "Tp0", "bnp", "ec", "Tvec",
+    "agp", "sqp", "w1", "wrg1_0", "vec_t", "p0b", "w2", "wrg2_1", "rcp", "wrg1_3",
+    "pv0", "wrg2_2", "zp", "wrg1_1", "pv1", "Tzp", "bnc2", "wrg1_2", "pv2", "TR0",
+    "bnc0", "pnact", "pv3", "TR2", "bnc1", "wrg2_3", "pv4", "bnc3", "CP0", "pv5",
+    "TR1", "vec_c", "wrg2_0", "pv6", "pnrg", "CP2", "pv7", "QW1", "sqc", "Qpn",
+    "CP1", "Mfp", "QP0", "TR4", "QW2", "M1_0", "rcc", "zc3", "zc2", "M1_1",
+    "QP2", "CP4", "zc1", "shared", "zc0", "M1_5", "AD0", "TR3", "AD1", "CP3",
+    "TR6", "QP1", "Tzc2", "AD5", "cact2", "Tzc1", "QP3", "cact1", "Tzc0", "QX0",
+    "M1_3", "cact0", "Tzc3", "AD3", "cact3", "crg0", "M1_4", "AD4", "crg1", "M1_7",
+    "AD7", "CP6", "TR5", "CP5", "M1_2", "AD2", "TR7", "Qc", "CP7", "M1_6",
+    "QP4", "M2_1", "QP6", "CO1", "M2_0", "QX1", "CO0", "ST0", "M1_12", "QX2",
+    "M2_2", "AD6", "CO2", "M1_9", "QP5", "M2_3", "AD12", "CO3", "ST1", "M1_8",
+    "AD9", "M2_5", "QX3", "CO5", "M1_10", "AD8", "M2_4", "QP7", "CO4", "ST2",
+    "M1_11", "QX4", "M2_6", "AD10", "CO6", "M1_13", "AD11", "M2_7", "QX5", "CO7",
+    "ST3", "M2_9", "AD13", "CO9", "M1_14", "QX6", "M2_8", "AD14", "CO8", "ST4",
+    "M1_15", "AD15", "M2_10", "QX7", "CO10", "M2_11", "CO11", "ST5", "M2_13", "CO13",
+    "M2_12", "CO12", "ST6", "M2_14", "CO14", "M2_15", "CO15", "ST7",
+)
+
+
+def tile_tromptcell_pa_kernel(
+    tc, prev_cell_out, emb_prompt, ln_prompt_w, ln_prompt_b, w_imp, b_imp, emb_column, ln_col_w, ln_col_b, out
+):
+    nc = tc.nc
+    with ExitStack() as ctx:
+        keep = ctx.enter_context(tc.tile_pool(name="keep", bufs=1))
+        ps_tr = ctx.enter_context(tc.psum_pool(name="ps_tr", bufs=2))
+        ps_s1 = ctx.enter_context(tc.psum_pool(name="ps_s1", bufs=3))
+        ps_s2 = ctx.enter_context(tc.psum_pool(name="ps_s2", bufs=3))
+        ctx.enter_context(tc.manual_schedule())
+
+        live = {}
+        steps = {}
+
+        def eng_of(name):
+            return ENG.get(name, "V")
+
+        def move(name, dst, src):
+            e = eng_of(name)
+            if e == "V":
+                nc.vector.tensor_copy(out=dst, in_=src)
+            elif e == "S":
+                nc.scalar.copy(out=dst, in_=src)
+            else:
+                nc.gpsimd.tensor_scalar(out=dst, in0=src, scalar1=1.0, scalar2=0.0, op0=ALU.mult, op1=ALU.add)
+
+        def affine(name, dst, src, scale, bias):
+            if eng_of(name) == "S":
+                nc.scalar.activation(out=dst, in_=src, func=ACT.Identity, scale=scale, bias=bias)
+            else:
+                nc.vector.tensor_scalar(out=dst, in0=src, scalar1=scale, scalar2=bias, op0=ALU.mult, op1=ALU.add)
+
+        vec_rows = keep.tile([P, P], BF16)
+        one_t = keep.tile([P, 1], F32)
+        warm = keep.tile([P, 1], F32)
+        ident_b = keep.tile([P, P], BF16)
+        ident_f = keep.tile([P, P], F32)
+        p0 = keep.tile([P, D], BF16)
+        ec = keep.tile([P, T, D], BF16)
+        w_raw = [keep.tile([P, T, D], BF16, name="wraw%d" % h) for h in range(2)]
+        prev_sb = [keep.tile([P, CH, D], BF16, name="prev%d" % c) for c in range(NCH)]
+        vec_t = keep.tile([P, 5 * T], F32)
+        st_p = keep.tile([P, 6], F32)
+        mv_p = keep.tile([P, 2], F32)
+        ve_p = keep.tile([P, 1], F32)
+        std_p = keep.tile([P, 1], F32)
+        rstd_p = keep.tile([P, 1], F32)
+        z_p = keep.tile([P, D], F32)
+        pn_planes = keep.tile([P, T, P], BF16)
+        pn_g = keep.tile([P, P, T], BF16, align_bytes=64)
+        pn_c = keep.tile([P, P], U32, align_bytes=64)
+        pn_s = keep.tile([P, P], U8, align_bytes=64)
+        p0b = keep.tile([P, T, P], F32)
+        w_g = [keep.tile([P, D, T], BF16, name="wg%d" % h, align_bytes=64) for h in range(2)]
+        w_c = [keep.tile([P, D], U32, name="wc%d" % h, align_bytes=64) for h in range(2)]
+        w_s = [keep.tile([P, D], U8, name="ws%d" % h, align_bytes=64) for h in range(2)]
+        shared = keep.tile([P, P, T], F32)
+        st_c = keep.tile([P, T, 6], F32)
+        mv_c = keep.tile([P, T, 2], F32)
+        ve_c = keep.tile([P, T], F32)
+        std_c = keep.tile([P, T], F32)
+        rstd_c = keep.tile([P, T], F32)
+        negm_c = keep.tile([P, T], F32)
+        nmr_c = keep.tile([P, T], F32)
+        z_c = [keep.tile([P, D], F32, name="zc%d" % a) for a in range(T)]
+        col_planes = keep.tile([P, T, D], BF16)
+        col_g = keep.tile([P, D, T], BF16, align_bytes=64)
+        col_c = keep.tile([P, D], U32, align_bytes=64)
+        col_s = keep.tile([P, D], U8, align_bytes=64)
+        pv_g = [keep.tile([P, CH * P * 2], F32, name="pvg%d" % c, align_bytes=64) for c in range(NCH)]
+        pv_c = keep.tile([P, B * P], U32, align_bytes=64)
+        pv_s = keep.tile([P, B * P], U8, align_bytes=64)
+        x_g = [keep.tile([P, CH, P, T], BF16, name="xg%d" % c, align_bytes=64) for c in range(NCH)]
+        x_c = keep.tile([P, B * P], U32, align_bytes=64)
+        x_s = keep.tile([P, B * P], U8, align_bytes=64)
+        o_sb = [keep.tile([P, CH, D], F32, name="o%d" % c) for c in range(NCH)]
+
+        def s_ms():
+            nc.vector.memset(vec_rows[:], 0.0)
+            nc.vector.memset(one_t[:], 1.0)
+
+        def s_warm():
+            nc.scalar.activation(out=warm[:], in_=one_t[:], func=ACT.Sqrt)
+
+        def s_vec():
+            for v, vec in enumerate((ln_prompt_w, ln_prompt_b, b_imp, ln_col_w, ln_col_b)):
+                nc.sync.dma_start(out=vec_rows[T * v : T * v + T, :], in_=vec.rearrange("(t c) -> t c", c=P))
+
+        def s_ec():
+            nc.sync.dma_start(
+                out=ec[:].rearrange("q a d -> q (a d)"), in_=emb_column.rearrange("(q a) d -> q (a d)", a=T)
+            )
+
+        def s_w2():
+            nc.sync.dma_start(
+                out=w_raw[1][:].rearrange("q (u e) c -> q u (e c)", u=2),
+                in_=w_imp[D : 2 * D, :].rearrange("(u q e) c -> q u (e c)", u=2, e=2),
+            )
+
+        def s_pv(c):
+            nc.sync.dma_start(out=prev_sb[c][:], in_=prev_cell_out[CH * c : CH * c + CH].rearrange("n p d -> p n d"))
+
+        def s_tvec():
+            live["vt"] = ps_tr.tile([P, P], BF16, tag="tr", name="vt_ps")
+            nc.tensor.transpose(live["vt"][:], vec_rows[:], ident_b[:])
+
+        def s_agp():
+            nc.vector.bn_aggr(out=mv_p[:], in_=st_p[:])
+            nc.vector.tensor_scalar_add(out=ve_p[:], in0=mv_p[:, 1:2], scalar1=EPS)
+
+        def s_zp():
+            nc.vector.tensor_scalar(
+                out=z_p[:], in0=p0[:], scalar1=mv_p[:, 0:1], scalar2=rstd_p[:], op0=ALU.subtract, op1=ALU.mult
+            )
+
+        def s_tzp():
+            live["zp"] = ps_tr.tile([P, T, P], F32, tag="tr", name="zp_ps")
+            for t in range(T):
+                nc.tensor.transpose(live["zp"][:, t, :], z_p[:, t * P : (t + 1) * P], ident_f[:])
+
+        def s_pnact():
+            for t in range(T):
+                affine("pnact", pn_planes[:, t, :], live["zp"][:, t, :], vec_t[:, t : t + 1], vec_t[:, T + t : T + t + 1])
+
+        def s_tp0():
+            live["p0t"] = ps_tr.tile([P, T, P], BF16, tag="tr", name="p0t_ps")
+            for t in range(T):
+                nc.tensor.transpose(live["p0t"][:, t, :], p0[:, t * P : (t + 1) * P], ident_b[:])
+
+        def s_p0b():
+            if eng_of("p0b") == "S":
+                for t in range(T):
+                    nc.scalar.activation(
+                        out=p0b[:, t, :],
+                        in_=live["p0t"][:, t, :],
+                        func=ACT.Identity,
+                        bias=vec_t[:, 2 * T + t : 2 * T + t + 1],
+                        scale=1.0,
+                    )
+            else:
+                nc.vector.tensor_tensor(
+                    out=p0b[:],
+                    in0=live["p0t"][:],
+                    in1=vec_t[:, 2 * T : 3 * T].unsqueeze(2).to_broadcast([P, T, P]),
+                    op=ALU.add,
+                )
+
+        def regroup(name, grouped, planes, part, parts):
+            w = D // parts
+            cs = slice(part * w, (part + 1) * w)
+            move(
+                name,
+                grouped[:, cs, :].rearrange("p (c i) t -> p c t i", i=4),
+                planes[:, :, cs].rearrange("p t (c i) -> p c t i", i=4),
+            )
+
+        def quant(codes, scales, src):
+            nc.vector.quantize_mx(out=codes.bitcast(FP8X4), scales=scales, in_=src)
+
+        def mx(dst, lc, ls, rc, rs):
+            nc.tensor.matmul_mx(
+                out=dst, lhsT=lc.bitcast(FP8X4), lhsT_scale=ls, rhs=rc.bitcast(FP8X4), rhs_scale=rs, start=True, stop=True
+            )
+
+        def s_mfp():
+            live["fp"] = ps_s1.tile([P, T, P], F32, tag="s1", name="fp_ps")
+            for t in range(T):
+                ts = slice(t * P, (t + 1) * P)
+                mx(live["fp"][:, t, :], w_c[0][:, ts], w_s[0][:, ts], pn_c[:], pn_s[:])
+
+        def s_shared():
+            nc.vector.tensor_tensor(
+                out=shared[:],
+                in0=live["fp"][:].rearrange("p t r -> p r t"),
+                in1=p0b[:].rearrange("p t r -> p r t"),
+                op=ALU.add,
+            )
+
+        def s_bnc(a):
+            nc.vector.bn_stats(out=st_c[:, a, :], in_=ec[:, a, :])
+            nc.vector.bn_aggr(out=mv_c[:, a, :], in_=st_c[:, a, :])
+
+        def s_vec_c():
+            nc.vector.tensor_scalar_add(out=ve_c[:], in0=mv_c[:, :, 1], scalar1=EPS)
+            nc.vector.tensor_scalar_mul(out=negm_c[:], in0=mv_c[:, :, 0], scalar1=-1.0)
+
+        def s_rcc():
+            nc.vector.reciprocal(out=rstd_c[:], in_=std_c[:])
+            nc.vector.tensor_tensor(out=nmr_c[:], in0=negm_c[:], in1=rstd_c[:], op=ALU.mult)
+
+        def s_zc(a):
+            e = eng_of("zc%d" % a)
+            if e == "S":
+                nc.scalar.activation(
+                    out=z_c[a][:], in_=ec[:, a, :], func=ACT.Identity, scale=rstd_c[:, a : a + 1], bias=nmr_c[:, a : a + 1]
+                )
+            else:
+                (nc.vector if e == "V" else nc.gpsimd).tensor_scalar(
+                    out=z_c[a][:],
+                    in0=ec[:, a, :],
+                    scalar1=negm_c[:, a : a + 1],
+                    scalar2=rstd_c[:, a : a + 1],
+                    op0=ALU.add,
+                    op1=ALU.mult,
+                )
+
+        def s_tzc(t):
+            live["ct%d" % t] = ps_s2.tile([P, T, P], F32, tag="s2", name="ct_ps%d" % t)
+            for a in range(T):
+                nc.tensor.transpose(live["ct%d" % t][:, a, :], z_c[a][:, t * P : (t + 1) * P], ident_f[:])
+
+        def s_cact(t):
+            affine(
+                "cact%d" % t,
+                col_planes[:, t, :].rearrange("k (q a) -> k q a", a=T),
+                live["ct%d" % t][:].rearrange("k a q -> k q a"),
+                vec_t[:, 3 * T + t : 3 * T + t + 1],
+                vec_t[:, 4 * T + t : 4 * T + t + 1],
+            )
+
+        def s_tr(c):
+            words = prev_sb[c][:].rearrange("p s d -> p (s d)").bitcast(F32)
+            live["tr%d" % c] = ps_tr.tile([P, CH, 2, P], F32, tag="tr", name="tr_ps%d" % c)
+            for s in range(CH):
+                for u in range(2):
+                    lo = s * (D // 2) + u * P
+                    nc.tensor.transpose(live["tr%d" % c][:, s, u, :], words[:, lo : lo + P], ident_f[:])
+
+        def s_cp(c):
+            move(
+                "CP%d" % c,
+                pv_g[c][:].rearrange("p (s r u) -> p s r u", s=CH, u=2),
+                live["tr%d" % c][:].rearrange("p s u r -> p s r u"),
+            )
+
+        def s_qp(c):
+            cs = slice(c * CH * P, (c + 1) * CH * P)
+            quant(pv_c[:, cs], pv_s[:, cs], pv_g[c][:].bitcast(BF16))
+
+        def s_m1(n):
+            live["s1_%d" % n] = ps_s1.tile([P, T, P], F32, tag="s1", name="s1_ps%d" % n)
+            ns = slice(n * P, (n + 1) * P)
+            for t in range(T):
+                ts = slice(t * P, (t + 1) * P)
+                mx(live["s1_%d" % n][:, t, :], w_c[1][:, ts], w_s[1][:, ts], pv_c[:, ns], pv_s[:, ns])
+
+        def s_ad(n):
+            nc.vector.tensor_tensor(
+                out=x_g[n // CH][:, n % CH],
+                in0=live["s1_%d" % n][:].rearrange("p t r -> p r t"),
+                in1=shared[:],
+                op=ALU.add,
+            )
+
+        def s_qx(c):
+            cs = slice(c * CH * P, (c + 1) * CH * P)
+            quant(x_c[:, cs], x_s[:, cs], x_g[c][:].rearrange("p s r t -> p (s r t)"))
+
+        def s_m2(n):
+            live["s2_%d" % n] = ps_s2.tile([P, D], F32, tag="s2", name="s2_ps%d" % n)
+            ns = slice(n * P, (n + 1) * P)
+            mx(live["s2_%d" % n][:], x_c[:, ns], x_s[:, ns], col_c[:], col_s[:])
+
+        def s_st(c):
+            nc.sync.dma_start(out=out[CH * c : CH * c + CH].rearrange("n p c -> p n c"), in_=o_sb[c][:])
+
+        steps["ms"] = s_ms
+        steps["warm"] = s_warm
+        steps["idb"] = lambda: make_identity(nc, ident_b[:])
+        steps["idf"] = lambda: make_identity(nc, ident_f[:])
+        steps["vec"] = s_vec
+        steps["p0"] = lambda: nc.sync.dma_start(out=p0[:], in_=emb_prompt)
+        steps["ec"] = s_ec
+        steps["w1"] = lambda: nc.sync.dma_start(out=w_raw[0][:], in_=w_imp[0:D, :].rearrange("(t p) e -> p t e", p=P))
+        steps["w2"] = s_w2
+        steps["Tvec"] = s_tvec
+        steps["vec_t"] = lambda: nc.vector.tensor_copy(out=vec_t[:], in_=live["vt"][:, 0 : 5 * T])
+        steps["bnp"] = lambda: nc.vector.bn_stats(out=st_p[:], in_=p0[:])
+        steps["agp"] = s_agp
+        steps["sqp"] = lambda: nc.scalar.activation(out=std_p[:], in_=ve_p[:], func=ACT.Sqrt)
+        steps["rcp"] = lambda: nc.vector.reciprocal(out=rstd_p[:], in_=std_p[:])
+        steps["zp"] = s_zp
+        steps["Tzp"] = s_tzp
+        steps["pnact"] = s_pnact
+        steps["pnrg"] = lambda: nc.vector.tensor_copy(out=pn_g[:], in_=pn_planes[:].rearrange("p t r -> p r t"))
+        steps["Qpn"] = lambda: quant(pn_c[:], pn_s[:], pn_g[:].rearrange("p r t -> p (r t)"))
+        steps["Tp0"] = s_tp0
+        steps["p0b"] = s_p0b
+        steps["Mfp"] = s_mfp
+        steps["shared"] = s_shared
+        steps["vec_c"] = s_vec_c
+        steps["sqc"] = lambda: nc.scalar.activation(out=std_c[:], in_=ve_c[:], func=ACT.Sqrt)
+        steps["rcc"] = s_rcc
+        steps["Qc"] = lambda: quant(col_c[:], col_s[:], col_g[:].rearrange("p c t -> p (c t)"))
+        for h, parts in ((0, WP1), (1, WP2)):
+            for i in range(parts):
+                steps["wrg%d_%d" % (h + 1, i)] = lambda h=h, i=i, parts=parts: regroup(
+                    "wrg%d_%d" % (h + 1, i), w_g[h], w_raw[h], i, parts
+                )
+            steps["QW%d" % (h + 1)] = lambda h=h: quant(w_c[h][:], w_s[h][:], w_g[h][:].rearrange("p c t -> p (c t)"))
+        for i in range(CPARTS):
+            steps["crg%d" % i] = lambda i=i: regroup("crg%d" % i, col_g, col_planes, i, CPARTS)
+        for a in range(T):
+            steps["bnc%d" % a] = lambda a=a: s_bnc(a)
+            steps["zc%d" % a] = lambda a=a: s_zc(a)
+            steps["Tzc%d" % a] = lambda a=a: s_tzc(a)
+            steps["cact%d" % a] = lambda a=a: s_cact(a)
+        for c in range(NCH):
+            steps["pv%d" % c] = lambda c=c: s_pv(c)
+            steps["TR%d" % c] = lambda c=c: s_tr(c)
+            steps["CP%d" % c] = lambda c=c: s_cp(c)
+            steps["QP%d" % c] = lambda c=c: s_qp(c)
+            steps["QX%d" % c] = lambda c=c: s_qx(c)
+            steps["ST%d" % c] = lambda c=c: s_st(c)
+        for n in range(B):
+            steps["M1_%d" % n] = lambda n=n: s_m1(n)
+            steps["AD%d" % n] = lambda n=n: s_ad(n)
+            steps["M2_%d" % n] = lambda n=n: s_m2(n)
+            steps["CO%d" % n] = lambda n=n: move("CO%d" % n, o_sb[n // CH][:, n % CH, :], live["s2_%d" % n][:])
+
+        assert len(ORDER) == len(steps)
+        for name in ORDER:
+            steps[name]()

@@ -26,65 +26,61 @@ FLOPS = 2 * P * D * D + 2 * 2 * B * P * D * D
 
 ENG = {
     "p0b": "S",
+    "wrg1_2": "S",
     "wrg1_3": "S",
     "wrg1_1": "S",
-    "wrg1_2": "S",
+    "wrg1_0": "S",
     "pnact": "S",
-    "wrg2_3": "S",
     "CP0": "S",
-    "wrg2_0": "S",
-    "CP2": "S",
-    "CP1": "S",
-    "zc3": "S",
-    "CP4": "S",
+    "wrg2_1": "S",
     "zc0": "S",
+    "zc1": "S",
+    "wrg2_0": "S",
     "CP3": "S",
-    "cact2": "S",
+    "CP4": "S",
+    "cact0": "S",
     "cact1": "S",
+    "CP2": "S",
     "cact3": "S",
+    "cact2": "S",
     "crg1": "S",
-    "CP6": "S",
+    "crg0": "S",
     "CP5": "S",
+    "CP6": "S",
     "CP7": "S",
-    "CO1": "S",
     "CO0": "S",
     "CO2": "S",
+    "CO7": "S",
+    "CO1": "S",
     "CO3": "S",
     "CO5": "S",
-    "CO4": "S",
     "CO6": "S",
-    "CO7": "S",
+    "CO4": "S",
     "CO9": "S",
     "CO8": "S",
-    "CO10": "S",
     "CO11": "S",
-    "CO13": "S",
+    "CO10": "S",
+    "CO12": "S",
     "CO15": "S",
-    "wrg1_0": "G",
-    "wrg2_1": "G",
-    "wrg2_2": "G",
-    "zc2": "G",
-    "zc1": "G",
-    "crg0": "G",
 }
 
 ORDER = (
-    "idf", "ms", "warm", "vec", "idb", "p0", "Tp0", "bnp", "ec", "Tvec",
-    "agp", "sqp", "w1", "wrg1_0", "vec_t", "p0b", "w2", "wrg2_1", "rcp", "wrg1_3",
-    "pv0", "wrg2_2", "zp", "wrg1_1", "pv1", "Tzp", "bnc2", "wrg1_2", "pv2", "TR0",
-    "bnc0", "pnact", "pv3", "TR2", "bnc1", "wrg2_3", "pv4", "bnc3", "CP0", "pv5",
-    "TR1", "vec_c", "wrg2_0", "pv6", "pnrg", "CP2", "pv7", "QW1", "sqc", "Qpn",
-    "CP1", "Mfp", "QP0", "TR4", "QW2", "M1_0", "rcc", "zc3", "zc2", "M1_1",
-    "QP2", "CP4", "zc1", "shared", "zc0", "M1_5", "AD0", "TR3", "AD1", "CP3",
-    "TR6", "QP1", "Tzc2", "AD5", "cact2", "Tzc1", "QP3", "cact1", "Tzc0", "QX0",
-    "M1_3", "cact0", "Tzc3", "AD3", "cact3", "crg0", "M1_4", "AD4", "crg1", "M1_7",
-    "AD7", "CP6", "TR5", "CP5", "M1_2", "AD2", "TR7", "Qc", "CP7", "M1_6",
-    "QP4", "M2_1", "QP6", "CO1", "M2_0", "QX1", "CO0", "ST0", "M1_12", "QX2",
-    "M2_2", "AD6", "CO2", "M1_9", "QP5", "M2_3", "AD12", "CO3", "ST1", "M1_8",
-    "AD9", "M2_5", "QX3", "CO5", "M1_10", "AD8", "M2_4", "QP7", "CO4", "ST2",
-    "M1_11", "QX4", "M2_6", "AD10", "CO6", "M1_13", "AD11", "M2_7", "QX5", "CO7",
-    "ST3", "M2_9", "AD13", "CO9", "M1_14", "QX6", "M2_8", "AD14", "CO8", "ST4",
-    "M1_15", "AD15", "M2_10", "QX7", "CO10", "M2_11", "CO11", "ST5", "M2_13", "CO13",
+    "idb", "ms", "warm", "vec", "idf", "Tvec", "p0", "Tp0", "bnp", "ec",
+    "agp", "sqp", "w1", "vec_t", "p0b", "w2", "bnc0", "wrg1_2", "pv0", "rcp",
+    "wrg1_3", "pv1", "bnc1", "wrg1_1", "pv2", "zp", "wrg1_0", "pv3", "Tzp", "bnc2",
+    "pnact", "pv4", "TR0", "bnc3", "pv5", "TR1", "vec_c", "sqc", "pv6", "wrg2_3",
+    "CP0", "pv7", "TR3", "QW1", "wrg2_1", "pnrg", "rcc", "zc0", "Qpn", "zc1",
+    "Mfp", "zc3", "wrg2_0", "CP1", "CP3", "TR4", "zc2", "CP4", "Tzc0", "wrg2_2",
+    "cact0", "Tzc1", "QP0", "cact1", "Tzc3", "QW2", "TR2", "QP3", "CP2", "M1_0",
+    "shared", "cact3", "M1_1", "QP1", "Tzc2", "QP4", "cact2", "M1_3", "AD0", "crg1",
+    "M1_6", "AD1", "crg0", "TR5", "QP2", "CP5", "M1_7", "AD3", "TR6", "AD6",
+    "CP6", "M1_2", "QX0", "M1_5", "AD7", "M1_4", "QX3", "TR7", "Qc", "CP7",
+    "M2_0", "AD2", "CO0", "M1_9", "QX1", "M2_2", "QP6", "CO2", "M2_7", "AD5",
+    "CO7", "M1_13", "QP5", "M2_1", "AD4", "CO1", "ST0", "M1_8", "QP7", "M2_3",
+    "QX2", "CO3", "ST1", "M2_5", "AD9", "CO5", "M1_11", "AD13", "M2_6", "AD8",
+    "CO6", "M1_10", "QX4", "M2_4", "AD11", "CO4", "ST2", "M1_12", "AD10", "ST3",
+    "M2_9", "QX5", "CO9", "M1_15", "AD12", "M2_8", "QX6", "CO8", "ST4", "M1_14",
+    "AD14", "M2_11", "AD15", "CO11", "M2_10", "QX7", "CO10", "ST5", "M2_13", "CO13",
     "M2_12", "CO12", "ST6", "M2_14", "CO14", "M2_15", "CO15", "ST7",
 )
 

@@ -25,63 +25,64 @@ CPARTS = 2
 FLOPS = 2 * P * D * D + 2 * 2 * B * P * D * D
 
 ENG = {
-    "p0b": "S",
     "wrg1_2": "S",
-    "wrg1_3": "S",
     "wrg1_1": "S",
-    "wrg1_0": "S",
-    "pnact": "S",
-    "CP0": "S",
-    "wrg2_1": "S",
-    "zc0": "S",
-    "zc1": "S",
     "wrg2_0": "S",
+    "pnact": "S",
+    "wrg2_3": "S",
+    "CP0": "S",
+    "CP1": "S",
+    "zc3": "S",
+    "zc2": "S",
     "CP3": "S",
     "CP4": "S",
     "cact0": "S",
+    "CP5": "S",
     "cact1": "S",
-    "CP2": "S",
-    "cact3": "S",
     "cact2": "S",
     "crg1": "S",
-    "crg0": "S",
-    "CP5": "S",
-    "CP6": "S",
     "CP7": "S",
+    "CP6": "S",
     "CO0": "S",
-    "CO2": "S",
-    "CO7": "S",
     "CO1": "S",
+    "CO2": "S",
     "CO3": "S",
     "CO5": "S",
-    "CO6": "S",
     "CO4": "S",
-    "CO9": "S",
+    "CO7": "S",
+    "CO6": "S",
     "CO8": "S",
-    "CO11": "S",
+    "CO9": "S",
     "CO10": "S",
+    "CO11": "S",
     "CO12": "S",
-    "CO15": "S",
+    "CO14": "S",
+    "wrg1_3": "G",
+    "wrg2_2": "G",
+    "wrg2_1": "G",
+    "zc0": "G",
+    "zc1": "G",
+    "crg0": "G",
 }
 
 ORDER = (
-    "idb", "ms", "warm", "vec", "idf", "Tvec", "p0", "Tp0", "bnp", "ec",
-    "agp", "sqp", "w1", "vec_t", "p0b", "w2", "bnc0", "wrg1_2", "pv0", "rcp",
-    "wrg1_3", "pv1", "bnc1", "wrg1_1", "pv2", "zp", "wrg1_0", "pv3", "Tzp", "bnc2",
-    "pnact", "pv4", "TR0", "bnc3", "pv5", "TR1", "vec_c", "sqc", "pv6", "wrg2_3",
-    "CP0", "pv7", "TR3", "QW1", "wrg2_1", "pnrg", "rcc", "zc0", "Qpn", "zc1",
-    "Mfp", "zc3", "wrg2_0", "CP1", "CP3", "TR4", "zc2", "CP4", "Tzc0", "wrg2_2",
-    "cact0", "Tzc1", "QP0", "cact1", "Tzc3", "QW2", "TR2", "QP3", "CP2", "M1_0",
-    "shared", "cact3", "M1_1", "QP1", "Tzc2", "QP4", "cact2", "M1_3", "AD0", "crg1",
-    "M1_6", "AD1", "crg0", "TR5", "QP2", "CP5", "M1_7", "AD3", "TR6", "AD6",
-    "CP6", "M1_2", "QX0", "M1_5", "AD7", "M1_4", "QX3", "TR7", "Qc", "CP7",
-    "M2_0", "AD2", "CO0", "M1_9", "QX1", "M2_2", "QP6", "CO2", "M2_7", "AD5",
-    "CO7", "M1_13", "QP5", "M2_1", "AD4", "CO1", "ST0", "M1_8", "QP7", "M2_3",
-    "QX2", "CO3", "ST1", "M2_5", "AD9", "CO5", "M1_11", "AD13", "M2_6", "AD8",
-    "CO6", "M1_10", "QX4", "M2_4", "AD11", "CO4", "ST2", "M1_12", "AD10", "ST3",
-    "M2_9", "QX5", "CO9", "M1_15", "AD12", "M2_8", "QX6", "CO8", "ST4", "M1_14",
-    "AD14", "M2_11", "AD15", "CO11", "M2_10", "QX7", "CO10", "ST5", "M2_13", "CO13",
-    "M2_12", "CO12", "ST6", "M2_14", "CO14", "M2_15", "CO15", "ST7",
+    "p0", "idf", "ms", "warm", "ec", "idb", "bnp", "vec", "Tvec", "agp",
+    "sqp", "w1", "wrg1_3", "Tp0", "bnc0", "wrg1_2", "w2", "wrg2_2", "rcp", "wrg1_1",
+    "pv0", "wrg2_1", "vec_t", "wrg2_0", "pv1", "zp", "pv2", "Tzp", "wrg1_0", "pnact",
+    "pv4", "p0b", "wrg2_3", "pv3", "TR0", "bnc2", "CP0", "pv5", "TR1", "bnc3",
+    "pv7", "TR2", "bnc1", "pv6", "vec_c", "sqc", "pnrg", "CP1", "TR3", "QW1",
+    "Qpn", "Mfp", "QW2", "rcc", "zc3", "zc0", "QP0", "zc2", "zc1", "M1_0",
+    "CP2", "CP3", "M1_1", "shared", "TR4", "QP1", "CP4", "Tzc0", "AD0", "cact0",
+    "TR5", "QP3", "CP5", "Tzc1", "AD1", "cact1", "M1_3", "QP2", "Tzc3", "QP4",
+    "Tzc2", "AD3", "cact2", "TR6", "cact3", "crg1", "crg0", "M1_5", "QP5", "M1_2",
+    "AD5", "M1_4", "AD2", "TR7", "AD4", "CP7", "M1_6", "QX0", "CP6", "M1_7",
+    "Qc", "M1_11", "QX1", "M2_0", "AD6", "CO0", "M2_1", "QX2", "CO1", "ST0",
+    "M1_9", "AD7", "M2_2", "AD11", "CO2", "M2_3", "QX3", "CO3", "ST1", "M1_8",
+    "QP6", "M2_5", "AD9", "CO5", "M1_10", "AD8", "M2_4", "QX4", "CO4", "ST2",
+    "M1_12", "QP7", "M2_7", "AD10", "CO7", "M2_6", "QX5", "CO6", "ST3", "M2_8",
+    "AD12", "CO8", "M1_13", "AD13", "M2_9", "QX6", "CO9", "ST4", "M1_14", "AD14",
+    "M2_10", "QXh14", "CO10", "M1_15", "AD15", "M2_11", "QXh15", "CO11", "ST5", "M2_12",
+    "CO12", "M2_13", "CO13", "ST6", "M2_14", "CO14", "STh14", "M2_15", "CO15", "STh15",
 )
 
 
@@ -89,6 +90,8 @@ def tile_tromptcell_pa_kernel(
     tc, prev_cell_out, emb_prompt, ln_prompt_w, ln_prompt_b, w_imp, b_imp, emb_column, ln_col_w, ln_col_b, out
 ):
     nc = tc.nc
+    pv_view = prev_cell_out.flatten_outer_dims().rearrange("(q j) d -> q j d", j=B)
+    out_view = out.flatten_outer_dims().rearrange("(q j) c -> q j c", j=B)
     with ExitStack() as ctx:
         keep = ctx.enter_context(tc.tile_pool(name="keep", bufs=1))
         ps_tr = ctx.enter_context(tc.psum_pool(name="ps_tr", bufs=2))
@@ -141,7 +144,7 @@ def tile_tromptcell_pa_kernel(
         w_g = [keep.tile([P, D, T], BF16, name="wg%d" % h, align_bytes=64) for h in range(2)]
         w_c = [keep.tile([P, D], U32, name="wc%d" % h, align_bytes=64) for h in range(2)]
         w_s = [keep.tile([P, D], U8, name="ws%d" % h, align_bytes=64) for h in range(2)]
-        shared = keep.tile([P, P, T], F32)
+        shared = keep.tile([P, B, P // B, T], F32)
         st_c = keep.tile([P, T, 6], F32)
         mv_c = keep.tile([P, T, 2], F32)
         ve_c = keep.tile([P, T], F32)
@@ -185,7 +188,7 @@ def tile_tromptcell_pa_kernel(
             )
 
         def s_pv(c):
-            nc.sync.dma_start(out=prev_sb[c][:], in_=prev_cell_out[CH * c : CH * c + CH].rearrange("n p d -> p n d"))
+            nc.sync.dma_start(out=prev_sb[c][:], in_=pv_view[:, CH * c : CH * c + CH, :])
 
         def s_tvec():
             live["vt"] = ps_tr.tile([P, P], BF16, tag="tr", name="vt_ps")
@@ -257,9 +260,9 @@ def tile_tromptcell_pa_kernel(
 
         def s_shared():
             nc.vector.tensor_tensor(
-                out=shared[:],
-                in0=live["fp"][:].rearrange("p t r -> p r t"),
-                in1=p0b[:].rearrange("p t r -> p r t"),
+                out=shared[:].rearrange("p j i t -> p i j t"),
+                in0=live["fp"][:].rearrange("p t (i j) -> p i j t", j=B),
+                in1=p0b[:].rearrange("p t (i j) -> p i j t", j=B),
                 op=ALU.add,
             )
 
@@ -333,9 +336,9 @@ def tile_tromptcell_pa_kernel(
 
         def s_ad(n):
             nc.vector.tensor_tensor(
-                out=x_g[n // CH][:, n % CH],
-                in0=live["s1_%d" % n][:].rearrange("p t r -> p r t"),
-                in1=shared[:],
+                out=x_g[n // CH][:, n % CH].rearrange("p (m i) t -> p m i t", m=B),
+                in0=live["s1_%d" % n][:].rearrange("p t (m i) -> p m i t", m=B),
+                in1=shared[:, n].unsqueeze(1).to_broadcast([P, B, P // B, T]),
                 op=ALU.add,
             )
 
@@ -349,7 +352,14 @@ def tile_tromptcell_pa_kernel(
             mx(live["s2_%d" % n][:], x_c[:, ns], x_s[:, ns], col_c[:], col_s[:])
 
         def s_st(c):
-            nc.sync.dma_start(out=out[CH * c : CH * c + CH].rearrange("n p c -> p n c"), in_=o_sb[c][:])
+            nc.sync.dma_start(out=out_view[:, CH * c : CH * c + CH, :], in_=o_sb[c][:])
+
+        def s_sth(n):
+            nc.sync.dma_start(out=out_view[:, n, :], in_=o_sb[n // CH][:, n % CH, :])
+
+        def s_qxh(n):
+            ns = slice(n * P, (n + 1) * P)
+            quant(x_c[:, ns], x_s[:, ns], x_g[n // CH][:, n % CH].rearrange("p r t -> p (r t)"))
 
         steps["ms"] = s_ms
         steps["warm"] = s_warm
@@ -397,8 +407,12 @@ def tile_tromptcell_pa_kernel(
             steps["TR%d" % c] = lambda c=c: s_tr(c)
             steps["CP%d" % c] = lambda c=c: s_cp(c)
             steps["QP%d" % c] = lambda c=c: s_qp(c)
+        for c in range(NCH - 1):
             steps["QX%d" % c] = lambda c=c: s_qx(c)
             steps["ST%d" % c] = lambda c=c: s_st(c)
+        for n in (B - 2, B - 1):
+            steps["QXh%d" % n] = lambda n=n: s_qxh(n)
+            steps["STh%d" % n] = lambda n=n: s_sth(n)
         for n in range(B):
             steps["M1_%d" % n] = lambda n=n: s_m1(n)
             steps["AD%d" % n] = lambda n=n: s_ad(n)

@@ -25,64 +25,67 @@ CPARTS = 2
 FLOPS = 2 * P * D * D + 2 * 2 * B * P * D * D
 
 ENG = {
+    "p0b": "S",
+    "zp": "S",
     "wrg1_2": "S",
-    "wrg1_1": "S",
-    "wrg2_0": "S",
+    "wrg1_0": "S",
     "pnact": "S",
+    "pnrg": "S",
     "wrg2_3": "S",
     "CP0": "S",
     "CP1": "S",
-    "zc3": "S",
+    "zc0": "S",
+    "CP2": "S",
     "zc2": "S",
     "CP3": "S",
-    "CP4": "S",
     "cact0": "S",
-    "CP5": "S",
     "cact1": "S",
-    "cact2": "S",
+    "CP4": "S",
+    "cact3": "S",
     "crg1": "S",
-    "CP7": "S",
+    "CP5": "S",
     "CP6": "S",
+    "CP7": "S",
     "CO0": "S",
     "CO1": "S",
     "CO2": "S",
     "CO3": "S",
-    "CO5": "S",
     "CO4": "S",
+    "CO5": "S",
     "CO7": "S",
     "CO6": "S",
     "CO8": "S",
     "CO9": "S",
-    "CO10": "S",
     "CO11": "S",
+    "CO10": "S",
     "CO12": "S",
     "CO14": "S",
-    "wrg1_3": "G",
-    "wrg2_2": "G",
+    "wrg1_1": "G",
     "wrg2_1": "G",
-    "zc0": "G",
     "zc1": "G",
+    "zc3": "G",
     "crg0": "G",
 }
 
 ORDER = (
-    "p0", "idf", "ms", "warm", "ec", "idb", "bnp", "vec", "Tvec", "agp",
-    "sqp", "w1", "wrg1_3", "Tp0", "bnc0", "wrg1_2", "w2", "wrg2_2", "rcp", "wrg1_1",
-    "pv0", "wrg2_1", "vec_t", "wrg2_0", "pv1", "zp", "pv2", "Tzp", "wrg1_0", "pnact",
-    "pv4", "p0b", "wrg2_3", "pv3", "TR0", "bnc2", "CP0", "pv5", "TR1", "bnc3",
-    "pv7", "TR2", "bnc1", "pv6", "vec_c", "sqc", "pnrg", "CP1", "TR3", "QW1",
-    "Qpn", "Mfp", "QW2", "rcc", "zc3", "zc0", "QP0", "zc2", "zc1", "M1_0",
-    "CP2", "CP3", "M1_1", "shared", "TR4", "QP1", "CP4", "Tzc0", "AD0", "cact0",
-    "TR5", "QP3", "CP5", "Tzc1", "AD1", "cact1", "M1_3", "QP2", "Tzc3", "QP4",
-    "Tzc2", "AD3", "cact2", "TR6", "cact3", "crg1", "crg0", "M1_5", "QP5", "M1_2",
-    "AD5", "M1_4", "AD2", "TR7", "AD4", "CP7", "M1_6", "QX0", "CP6", "M1_7",
-    "Qc", "M1_11", "QX1", "M2_0", "AD6", "CO0", "M2_1", "QX2", "CO1", "ST0",
-    "M1_9", "AD7", "M2_2", "AD11", "CO2", "M2_3", "QX3", "CO3", "ST1", "M1_8",
-    "QP6", "M2_5", "AD9", "CO5", "M1_10", "AD8", "M2_4", "QX4", "CO4", "ST2",
-    "M1_12", "QP7", "M2_7", "AD10", "CO7", "M2_6", "QX5", "CO6", "ST3", "M2_8",
-    "AD12", "CO8", "M1_13", "AD13", "M2_9", "QX6", "CO9", "ST4", "M1_14", "AD14",
-    "M2_10", "QXh14", "CO10", "M1_15", "AD15", "M2_11", "QXh15", "CO11", "ST5", "M2_12",
-    "CO12", "M2_13", "CO13", "ST6", "M2_14", "CO14", "STh14", "M2_15", "CO15", "STh15",
+    "p0", "idf", "ms", "warm", "vec", "idb", "Tvec", "bnp", "ec", "Tp0",
+    "agp", "sqp", "w1", "wrg1_1", "vec_t", "p0b", "w2", "wrg2_1", "rcp", "zp",
+    "pv0", "Tzp", "bnc3", "wrg1_2", "pv1", "TR0", "bnc2", "wrg1_0", "pv2", "bnc0",
+    "pnact", "pv6", "TR1", "vecc1", "pnrg", "pv4", "wrg1_3", "wrg2_3", "pv7", "bnc1",
+    "CP0", "pv3", "TR2", "vecc0", "sqc0", "pv5", "QW1", "CP1", "wrg2_2", "sqc1",
+    "wrg2_0", "Qpn", "Mfp", "QW2", "QP0", "M1_0", "rcc0", "zc0", "zc1", "M1_1",
+    "QP1", "CP2", "TR3", "rcc1", "zc2", "zc3", "Tzc0", "shared", "CP3", "Tzc1",
+    "AD0", "cact0", "M1_2", "AD1", "cact1", "crg0", "M1_3", "QP2", "Tzc2", "QX0",
+    "TR4", "QP3", "CP4", "Tzc3", "AD2", "cact3", "M1_4", "cact2", "crg1", "M1_5",
+    "AD3", "TR5", "AD4", "CP5", "M1_7", "QP4", "M1_6", "Qc0", "TR6", "AD5",
+    "CP6", "TR7", "Qc1", "CP7", "M2_0", "QX1", "CO0", "M2_1", "QX2", "CO1",
+    "ST0", "M2_3", "AD7", "M1_8", "AD6", "M2_2", "QP5", "CO2", "M1_9", "QX3",
+    "CO3", "ST1", "M1_10", "QP6", "M2_4", "AD8", "CO4", "M2_5", "AD9", "CO5",
+    "ST2", "M1_11", "AD10", "M2_6", "QX4", "M2_7", "AD11", "CO7", "M1_12", "QX5",
+    "CO6", "ST3", "M1_13", "QP7", "M2_8", "AD12", "CO8", "M2_9", "AD13", "CO9",
+    "ST4", "M2_11", "QX6", "CO11", "M1_15", "AD15", "M1_14", "AD14", "M2_10", "QXh14",
+    "CO10", "ST5", "M2_13", "QXh15", "M2_12", "CO13", "CO12", "ST6", "M2_14", "CO14",
+    "STh14", "M2_15", "CO15", "STh15",
 )
 
 
@@ -135,6 +138,7 @@ def tile_tromptcell_pa_kernel(
         ve_p = keep.tile([P, 1], F32)
         std_p = keep.tile([P, 1], F32)
         rstd_p = keep.tile([P, 1], F32)
+        nmr_p = keep.tile([P, 1], F32)
         z_p = keep.tile([P, D], F32)
         pn_planes = keep.tile([P, T, P], BF16)
         pn_g = keep.tile([P, P, T], BF16, align_bytes=64)
@@ -177,9 +181,7 @@ def tile_tromptcell_pa_kernel(
                 nc.sync.dma_start(out=vec_rows[T * v : T * v + T, :], in_=vec.rearrange("(t c) -> t c", c=P))
 
         def s_ec():
-            nc.sync.dma_start(
-                out=ec[:].rearrange("q a d -> q (a d)"), in_=emb_column.rearrange("(q a) d -> q (a d)", a=T)
-            )
+            nc.sync.dma_start(out=ec[:], in_=emb_column.rearrange("(a q) d -> q a d", q=P))
 
         def s_w2():
             nc.sync.dma_start(
@@ -198,10 +200,19 @@ def tile_tromptcell_pa_kernel(
             nc.vector.bn_aggr(out=mv_p[:], in_=st_p[:])
             nc.vector.tensor_scalar_add(out=ve_p[:], in0=mv_p[:, 1:2], scalar1=EPS)
 
-        def s_zp():
-            nc.vector.tensor_scalar(
-                out=z_p[:], in0=p0[:], scalar1=mv_p[:, 0:1], scalar2=rstd_p[:], op0=ALU.subtract, op1=ALU.mult
+        def s_rcp():
+            nc.vector.reciprocal(out=rstd_p[:], in_=std_p[:])
+            nc.vector.scalar_tensor_tensor(
+                out=nmr_p[:], in0=mv_p[:, 0:1], scalar=-1.0, in1=rstd_p[:], op0=ALU.mult, op1=ALU.mult
             )
+
+        def s_zp():
+            if eng_of("zp") == "S":
+                nc.scalar.activation(out=z_p[:], in_=p0[:], func=ACT.Identity, scale=rstd_p[:], bias=nmr_p[:])
+            else:
+                nc.vector.tensor_scalar(
+                    out=z_p[:], in0=p0[:], scalar1=mv_p[:, 0:1], scalar2=rstd_p[:], op0=ALU.subtract, op1=ALU.mult
+                )
 
         def s_tzp():
             live["zp"] = ps_tr.tile([P, T, P], F32, tag="tr", name="zp_ps")
@@ -270,13 +281,23 @@ def tile_tromptcell_pa_kernel(
             nc.vector.bn_stats(out=st_c[:, a, :], in_=ec[:, a, :])
             nc.vector.bn_aggr(out=mv_c[:, a, :], in_=st_c[:, a, :])
 
-        def s_vec_c():
-            nc.vector.tensor_scalar_add(out=ve_c[:], in0=mv_c[:, :, 1], scalar1=EPS)
-            nc.vector.tensor_scalar_mul(out=negm_c[:], in0=mv_c[:, :, 0], scalar1=-1.0)
+        def s_vecc(h):
+            hs = slice(2 * h, 2 * h + 2)
+            nc.vector.tensor_scalar_add(out=ve_c[:, hs], in0=mv_c[:, hs, 1], scalar1=EPS)
+            nc.vector.tensor_scalar_mul(out=negm_c[:, hs], in0=mv_c[:, hs, 0], scalar1=-1.0)
 
-        def s_rcc():
-            nc.vector.reciprocal(out=rstd_c[:], in_=std_c[:])
-            nc.vector.tensor_tensor(out=nmr_c[:], in0=negm_c[:], in1=rstd_c[:], op=ALU.mult)
+        def s_sqc(h):
+            hs = slice(2 * h, 2 * h + 2)
+            nc.scalar.activation(out=std_c[:, hs], in_=ve_c[:, hs], func=ACT.Sqrt)
+
+        def s_rcc(h):
+            hs = slice(2 * h, 2 * h + 2)
+            nc.vector.reciprocal(out=rstd_c[:, hs], in_=std_c[:, hs])
+            nc.vector.tensor_tensor(out=nmr_c[:, hs], in0=negm_c[:, hs], in1=rstd_c[:, hs], op=ALU.mult)
+
+        def s_qc(h):
+            cs = slice(h * D // 2, (h + 1) * D // 2)
+            quant(col_c[:, cs], col_s[:, cs], col_g[:, cs, :].rearrange("p c t -> p (c t)"))
 
         def s_zc(a):
             e = eng_of("zc%d" % a)
@@ -294,19 +315,25 @@ def tile_tromptcell_pa_kernel(
                     op1=ALU.mult,
                 )
 
-        def s_tzc(t):
-            live["ct%d" % t] = ps_s2.tile([P, T, P], F32, tag="s2", name="ct_ps%d" % t)
-            for a in range(T):
-                nc.tensor.transpose(live["ct%d" % t][:, a, :], z_c[a][:, t * P : (t + 1) * P], ident_f[:])
+        def s_tzc(i):
+            h, tp = i // 2, i % 2
+            live["ct%d" % i] = ps_s2.tile([P, 2, 2, P], F32, tag="s2", name="ct_ps%d" % i)
+            for tt in range(2):
+                t = 2 * tp + tt
+                for aa in range(2):
+                    nc.tensor.transpose(live["ct%d" % i][:, tt, aa, :], z_c[2 * h + aa][:, t * P : (t + 1) * P], ident_f[:])
 
-        def s_cact(t):
-            affine(
-                "cact%d" % t,
-                col_planes[:, t, :].rearrange("k (q a) -> k q a", a=T),
-                live["ct%d" % t][:].rearrange("k a q -> k q a"),
-                vec_t[:, 3 * T + t : 3 * T + t + 1],
-                vec_t[:, 4 * T + t : 4 * T + t + 1],
-            )
+        def s_cact(i):
+            h, tp = i // 2, i % 2
+            for tt in range(2):
+                t = 2 * tp + tt
+                affine(
+                    "cact%d" % i,
+                    col_planes[:, t, h * D // 2 : (h + 1) * D // 2],
+                    live["ct%d" % i][:, tt].rearrange("k a q -> k (a q)"),
+                    vec_t[:, 3 * T + t : 3 * T + t + 1],
+                    vec_t[:, 4 * T + t : 4 * T + t + 1],
+                )
 
         def s_tr(c):
             words = prev_sb[c][:].rearrange("p s d -> p (s d)").bitcast(F32)
@@ -347,7 +374,10 @@ def tile_tromptcell_pa_kernel(
             quant(x_c[:, cs], x_s[:, cs], x_g[c][:].rearrange("p s r t -> p (s r t)"))
 
         def s_m2(n):
-            live["s2_%d" % n] = ps_s2.tile([P, D], F32, tag="s2", name="s2_ps%d" % n)
+            if n % 5 < 3:
+                live["s2_%d" % n] = ps_s2.tile([P, D], F32, tag="s2", name="s2_ps%d" % n)
+            else:
+                live["s2_%d" % n] = ps_tr.tile([P, D], F32, tag="tr", name="s2_ps%d" % n)
             ns = slice(n * P, (n + 1) * P)
             mx(live["s2_%d" % n][:], x_c[:, ns], x_s[:, ns], col_c[:], col_s[:])
 
@@ -375,20 +405,21 @@ def tile_tromptcell_pa_kernel(
         steps["bnp"] = lambda: nc.vector.bn_stats(out=st_p[:], in_=p0[:])
         steps["agp"] = s_agp
         steps["sqp"] = lambda: nc.scalar.activation(out=std_p[:], in_=ve_p[:], func=ACT.Sqrt)
-        steps["rcp"] = lambda: nc.vector.reciprocal(out=rstd_p[:], in_=std_p[:])
+        steps["rcp"] = s_rcp
         steps["zp"] = s_zp
         steps["Tzp"] = s_tzp
         steps["pnact"] = s_pnact
-        steps["pnrg"] = lambda: nc.vector.tensor_copy(out=pn_g[:], in_=pn_planes[:].rearrange("p t r -> p r t"))
+        steps["pnrg"] = lambda: move("pnrg", pn_g[:], pn_planes[:].rearrange("p t r -> p r t"))
         steps["Qpn"] = lambda: quant(pn_c[:], pn_s[:], pn_g[:].rearrange("p r t -> p (r t)"))
         steps["Tp0"] = s_tp0
         steps["p0b"] = s_p0b
         steps["Mfp"] = s_mfp
         steps["shared"] = s_shared
-        steps["vec_c"] = s_vec_c
-        steps["sqc"] = lambda: nc.scalar.activation(out=std_c[:], in_=ve_c[:], func=ACT.Sqrt)
-        steps["rcc"] = s_rcc
-        steps["Qc"] = lambda: quant(col_c[:], col_s[:], col_g[:].rearrange("p c t -> p (c t)"))
+        for h in range(2):
+            steps["vecc%d" % h] = lambda h=h: s_vecc(h)
+            steps["sqc%d" % h] = lambda h=h: s_sqc(h)
+            steps["rcc%d" % h] = lambda h=h: s_rcc(h)
+            steps["Qc%d" % h] = lambda h=h: s_qc(h)
         for h, parts in ((0, WP1), (1, WP2)):
             for i in range(parts):
                 steps["wrg%d_%d" % (h + 1, i)] = lambda h=h, i=i, parts=parts: regroup(

@@ -13,79 +13,98 @@ ACT = mybir.ActivationFunctionType
 
 P = 128
 D = 512
-B = 16
-T = 4
+PACK = 4
+TILES = 16
+PAIR = 2
+PAIRS = TILES // PAIR
+PER_TILE = P // TILES
+QUARTERS = 4
+HALVES = 2
+HALF = D // HALVES
 EPS = 1e-5
-CH = 2
-NCH = B // CH
-WP1 = 4
-WP2 = 4
-CPARTS = 2
+N_VECTORS = 5
+LN_PROMPT_W = 0
+LN_PROMPT_B = 1
+B_IMP = 2
+LN_COL_W = 3
+LN_COL_B = 4
+BN_STATS = 6
+BN_AGGR = 2
+RUN = 4
+T_BANKS = 2
+X_BANKS = 3
+O_BANKS = 3
 
-FLOPS = 2 * P * D * D + 2 * 2 * B * P * D * D
+FLOPS = 2 * P * D * D + 2 * 2 * TILES * P * D * D
 
-ENG = {
-    "p0b": "S",
-    "zp": "S",
-    "wrg1_2": "S",
-    "wrg1_0": "S",
-    "pnact": "S",
-    "pnrg": "S",
-    "wrg2_3": "S",
-    "CP0": "S",
-    "CP1": "S",
-    "zc0": "S",
-    "CP2": "S",
-    "zc2": "S",
-    "CP3": "S",
-    "cact0": "S",
-    "cact1": "S",
-    "CP4": "S",
-    "cact3": "S",
-    "crg1": "S",
-    "CP5": "S",
-    "CP6": "S",
-    "CP7": "S",
-    "CO0": "S",
-    "CO1": "S",
-    "CO2": "S",
-    "CO3": "S",
-    "CO4": "S",
-    "CO5": "S",
-    "CO7": "S",
-    "CO6": "S",
-    "CO8": "S",
-    "CO9": "S",
-    "CO11": "S",
-    "CO10": "S",
-    "CO12": "S",
-    "CO14": "S",
-    "wrg1_1": "G",
-    "wrg2_1": "G",
-    "zc1": "G",
-    "zc3": "G",
-    "crg0": "G",
-}
+SYNC = "sync"
+GPSIMD = "gpsimd"
+TENSOR = "tensor"
+VECTOR = "vector"
+SCALAR = "scalar"
+ENGINES = (SYNC, GPSIMD, TENSOR, VECTOR, SCALAR)
 
-ORDER = (
-    "p0", "idf", "ms", "warm", "vec", "idb", "Tvec", "bnp", "ec", "Tp0",
-    "agp", "sqp", "w1", "wrg1_1", "vec_t", "p0b", "w2", "wrg2_1", "rcp", "zp",
-    "pv0", "Tzp", "bnc3", "wrg1_2", "pv1", "TR0", "bnc2", "wrg1_0", "pv2", "bnc0",
-    "pnact", "pv6", "TR1", "vecc1", "pnrg", "pv4", "wrg1_3", "wrg2_3", "pv7", "bnc1",
-    "CP0", "pv3", "TR2", "vecc0", "sqc0", "pv5", "QW1", "CP1", "wrg2_2", "sqc1",
-    "wrg2_0", "Qpn", "Mfp", "QW2", "QP0", "M1_0", "rcc0", "zc0", "zc1", "M1_1",
-    "QP1", "CP2", "TR3", "rcc1", "zc2", "zc3", "Tzc0", "shared", "CP3", "Tzc1",
-    "AD0", "cact0", "M1_2", "AD1", "cact1", "crg0", "M1_3", "QP2", "Tzc2", "QX0",
-    "TR4", "QP3", "CP4", "Tzc3", "AD2", "cact3", "M1_4", "cact2", "crg1", "M1_5",
-    "AD3", "TR5", "AD4", "CP5", "M1_7", "QP4", "M1_6", "Qc0", "TR6", "AD5",
-    "CP6", "TR7", "Qc1", "CP7", "M2_0", "QX1", "CO0", "M2_1", "QX2", "CO1",
-    "ST0", "M2_3", "AD7", "M1_8", "AD6", "M2_2", "QP5", "CO2", "M1_9", "QX3",
-    "CO3", "ST1", "M1_10", "QP6", "M2_4", "AD8", "CO4", "M2_5", "AD9", "CO5",
-    "ST2", "M1_11", "AD10", "M2_6", "QX4", "M2_7", "AD11", "CO7", "M1_12", "QX5",
-    "CO6", "ST3", "M1_13", "QP7", "M2_8", "AD12", "CO8", "M2_9", "AD13", "CO9",
-    "ST4", "M2_11", "QX6", "CO11", "M1_15", "AD15", "M1_14", "AD14", "M2_10", "QXh14",
-    "CO10", "ST5", "M2_13", "QXh15", "M2_12", "CO13", "CO12", "ST6", "M2_14", "CO14",
-    "STh14", "M2_15", "CO15", "STh15",
+SCHEDULE = (
+    ("load_prompt",    "identity_f32",    "",             "clear",           "sqrt_table"),
+    ("load_vectors",   "identity_bf16",   "T_vectors",    "p_stats",         ""),
+    ("load_column",    "",                "T_prompt",     "p_var",           "p_std"),
+    ("load_w0",        "w0_group1",       "",             "vectors",         "p_bias"),
+    ("load_w1",        "w1_group1",       "",             "p_rstd",          "p_norm"),
+    ("load_prev0",     "",                "T_p_norm",     "c_stats0",        "w0_group2"),
+    ("load_prev1",     "",                "T_prev0",      "c_stats1",        "w0_group0"),
+    ("load_prev2",     "",                "",             "c_var0",          "p_gain"),
+    ("load_prev3",     "",                "T_prev1",      "c_stats2",        "p_group"),
+    ("load_prev4",     "",                "",             "w0_group3",       "w1_group3"),
+    ("load_prev5",     "",                "",             "c_stats3",        "prev_copy0"),
+    ("load_prev6",     "",                "T_prev2",      "c_var1",          "c_std0"),
+    ("load_prev7",     "",                "",             "w0_quant",        "prev_copy1"),
+    ("",               "",                "",             "w1_group2",       "c_std1"),
+    ("",               "",                "",             "w1_group0",       ""),
+    ("",               "",                "",             "p_quant",         ""),
+    ("",               "",                "mm_prompt",    "w1_quant",        ""),
+    ("",               "",                "",             "prev_quant0",     ""),
+    ("",               "",                "mm_x0",        "c_rstd0",         "c_norm0"),
+    ("",               "c_norm1",         "mm_x1",        "prev_quant1",     "prev_copy2"),
+    ("",               "",                "T_prev3",      "c_rstd1",         "c_norm2"),
+    ("",               "c_norm3",         "T_c_norm0",    "shared",          "prev_copy3"),
+    ("",               "",                "T_c_norm1",    "x_add0",          "c_gain0"),
+    ("",               "",                "mm_x2",        "x_add1",          "c_gain1"),
+    ("",               "c_group0",        "mm_x3",        "prev_quant2",     ""),
+    ("",               "",                "T_c_norm2",    "x_quant0",        ""),
+    ("",               "",                "T_prev4",      "prev_quant3",     "prev_copy4"),
+    ("",               "",                "T_c_norm3",    "x_add2",          "c_gain3"),
+    ("",               "",                "mm_x4",        "c_gain2",         "c_group1"),
+    ("",               "",                "mm_x5",        "x_add3",          ""),
+    ("",               "",                "T_prev5",      "x_add4",          "prev_copy5"),
+    ("",               "",                "mm_x6",        "prev_quant4",     ""),
+    ("",               "",                "mm_x7",        "c_quant0",        ""),
+    ("",               "",                "T_prev6",      "x_add5",          "prev_copy6"),
+    ("",               "",                "T_prev7",      "c_quant1",        "prev_copy7"),
+    ("",               "",                "mm_out0",      "x_quant1",        "out_copy0"),
+    ("",               "",                "mm_out1",      "x_quant2",        "out_copy1"),
+    ("store0",         "",                "mm_out2",      "x_add6",          "out_copy2"),
+    ("",               "",                "mm_x8",        "x_add7",          ""),
+    ("",               "",                "mm_out3",      "prev_quant5",     "out_copy3"),
+    ("store1",         "",                "mm_x9",        "x_quant3",        ""),
+    ("",               "",                "mm_x10",       "prev_quant6",     ""),
+    ("",               "",                "mm_out4",      "x_add8",          "out_copy4"),
+    ("",               "",                "mm_out5",      "x_add9",          "out_copy5"),
+    ("store2",         "",                "mm_x11",       "x_add10",         ""),
+    ("",               "",                "mm_out6",      "x_quant4",        "out_copy6"),
+    ("",               "",                "mm_out7",      "x_add11",         "out_copy7"),
+    ("store3",         "",                "mm_x12",       "x_quant5",        ""),
+    ("",               "",                "mm_x13",       "prev_quant7",     ""),
+    ("",               "",                "mm_out8",      "x_add12",         "out_copy8"),
+    ("",               "",                "mm_out9",      "x_add13",         "out_copy9"),
+    ("store4",         "",                "mm_out10",     "x_quant6",        "out_copy10"),
+    ("",               "",                "mm_x14",       "x_add14",         ""),
+    ("",               "",                "mm_x15",       "x_add15",         ""),
+    ("",               "",                "mm_out11",     "x_quant_tile14",  "out_copy11"),
+    ("store5",         "",                "mm_out12",     "x_quant_tile15",  "out_copy12"),
+    ("",               "",                "mm_out13",     "out_copy13",      ""),
+    ("store6",         "",                "mm_out14",     "",                "out_copy14"),
+    ("store_tile14",   "",                "mm_out15",     "out_copy15",      ""),
+    ("store_tile15",   "",                "",             "",                ""),
 )
 
 
@@ -93,363 +112,449 @@ def tile_tromptcell_pa_kernel(
     tc, prev_cell_out, emb_prompt, ln_prompt_w, ln_prompt_b, w_imp, b_imp, emb_column, ln_col_w, ln_col_b, out
 ):
     nc = tc.nc
-    pv_view = prev_cell_out.flatten_outer_dims().rearrange("(q j) d -> q j d", j=B)
-    out_view = out.flatten_outer_dims().rearrange("(q j) c -> q j c", j=B)
+    prev_rows = prev_cell_out.flatten_outer_dims().rearrange("(q j) d -> q j d", j=TILES)
+    out_rows = out.flatten_outer_dims().rearrange("(q j) c -> q j c", j=TILES)
+
     with ExitStack() as ctx:
         keep = ctx.enter_context(tc.tile_pool(name="keep", bufs=1))
-        ps_tr = ctx.enter_context(tc.psum_pool(name="ps_tr", bufs=2))
-        ps_s1 = ctx.enter_context(tc.psum_pool(name="ps_s1", bufs=3))
-        ps_s2 = ctx.enter_context(tc.psum_pool(name="ps_s2", bufs=3))
+        ps_t = ctx.enter_context(tc.psum_pool(name="ps_t", bufs=T_BANKS))
+        ps_x = ctx.enter_context(tc.psum_pool(name="ps_x", bufs=X_BANKS))
+        ps_o = ctx.enter_context(tc.psum_pool(name="ps_o", bufs=O_BANKS))
         ctx.enter_context(tc.manual_schedule())
 
-        live = {}
+        vector_rows = keep.tile([P, P], BF16)
+        vectors = keep.tile([P, N_VECTORS * PACK], F32)
+        one = keep.tile([P, 1], F32)
+        sqrt_of_one = keep.tile([P, 1], F32)
+        identity_bf16 = keep.tile([P, P], BF16)
+        identity_f32 = keep.tile([P, P], F32)
+
+        prompt = keep.tile([P, D], BF16)
+        p_stats = keep.tile([P, BN_STATS], F32)
+        p_mean_var = keep.tile([P, BN_AGGR], F32)
+        p_var_eps = keep.tile([P, 1], F32)
+        p_std = keep.tile([P, 1], F32)
+        p_rstd = keep.tile([P, 1], F32)
+        p_shift = keep.tile([P, 1], F32)
+        p_norm = keep.tile([P, D], F32)
+        pn_planes = keep.tile([P, PACK, P], BF16)
+        pn_grouped = keep.tile([P, P, PACK], BF16, align_bytes=64)
+        pn_words = keep.tile([P, P], U32, align_bytes=64)
+        pn_scales = keep.tile([P, P], U8, align_bytes=64)
+        prompt_bias = keep.tile([P, PACK, P], F32)
+        shared = keep.tile([P, TILES, PER_TILE, PACK], F32)
+
+        w_raw = [keep.tile([P, PACK, D], BF16, name="w_raw%d" % h) for h in range(2)]
+        w_grouped = [keep.tile([P, D, PACK], BF16, name="w_grouped%d" % h, align_bytes=64) for h in range(2)]
+        w_words = [keep.tile([P, D], U32, name="w_words%d" % h, align_bytes=64) for h in range(2)]
+        w_scales = [keep.tile([P, D], U8, name="w_scales%d" % h, align_bytes=64) for h in range(2)]
+
+        emb_col = keep.tile([P, PACK, D], BF16)
+        c_stats = keep.tile([P, PACK, BN_STATS], F32)
+        c_mean_var = keep.tile([P, PACK, BN_AGGR], F32)
+        c_var_eps = keep.tile([P, PACK], F32)
+        c_std = keep.tile([P, PACK], F32)
+        c_rstd = keep.tile([P, PACK], F32)
+        c_neg_mean = keep.tile([P, PACK], F32)
+        c_shift = keep.tile([P, PACK], F32)
+        c_norm = [keep.tile([P, D], F32, name="c_norm%d" % a) for a in range(PACK)]
+        col_planes = keep.tile([P, PACK, D], BF16)
+        col_grouped = keep.tile([P, D, PACK], BF16, align_bytes=64)
+        col_words = keep.tile([P, D], U32, align_bytes=64)
+        col_scales = keep.tile([P, D], U8, align_bytes=64)
+
+        prev = [keep.tile([P, PAIR, D], BF16, name="prev%d" % c) for c in range(PAIRS)]
+        prev_grouped = [
+            keep.tile([P, PAIR * P * 2], F32, name="prev_grouped%d" % c, align_bytes=64) for c in range(PAIRS)
+        ]
+        prev_words = keep.tile([P, TILES * P], U32, align_bytes=64)
+        prev_scales = keep.tile([P, TILES * P], U8, align_bytes=64)
+        x_grouped = [keep.tile([P, PAIR, P, PACK], BF16, name="x_grouped%d" % c, align_bytes=64) for c in range(PAIRS)]
+        x_words = keep.tile([P, TILES * P], U32, align_bytes=64)
+        x_scales = keep.tile([P, TILES * P], U8, align_bytes=64)
+        result = [keep.tile([P, PAIR, D], F32, name="result%d" % c) for c in range(PAIRS)]
+
+        banks = {}
         steps = {}
 
-        def eng_of(name):
-            return ENG.get(name, "V")
+        def step(name, engines, emit):
+            steps[name] = (engines, emit)
 
-        def move(name, dst, src):
-            e = eng_of(name)
-            if e == "V":
+        def copy_bits(engine, dst, src):
+            if engine == VECTOR:
                 nc.vector.tensor_copy(out=dst, in_=src)
-            elif e == "S":
+            elif engine == SCALAR:
                 nc.scalar.copy(out=dst, in_=src)
             else:
                 nc.gpsimd.tensor_scalar(out=dst, in0=src, scalar1=1.0, scalar2=0.0, op0=ALU.mult, op1=ALU.add)
 
-        def affine(name, dst, src, scale, bias):
-            if eng_of(name) == "S":
-                nc.scalar.activation(out=dst, in_=src, func=ACT.Identity, scale=scale, bias=bias)
+        def gain_and_bias(engine, dst, src, gain, bias):
+            if engine == SCALAR:
+                nc.scalar.activation(out=dst, in_=src, func=ACT.Identity, scale=gain, bias=bias)
             else:
-                nc.vector.tensor_scalar(out=dst, in0=src, scalar1=scale, scalar2=bias, op0=ALU.mult, op1=ALU.add)
+                nc.vector.tensor_scalar(out=dst, in0=src, scalar1=gain, scalar2=bias, op0=ALU.mult, op1=ALU.add)
 
-        vec_rows = keep.tile([P, P], BF16)
-        one_t = keep.tile([P, 1], F32)
-        warm = keep.tile([P, 1], F32)
-        ident_b = keep.tile([P, P], BF16)
-        ident_f = keep.tile([P, P], F32)
-        p0 = keep.tile([P, D], BF16)
-        ec = keep.tile([P, T, D], BF16)
-        w_raw = [keep.tile([P, T, D], BF16, name="wraw%d" % h) for h in range(2)]
-        prev_sb = [keep.tile([P, CH, D], BF16, name="prev%d" % c) for c in range(NCH)]
-        vec_t = keep.tile([P, 5 * T], F32)
-        st_p = keep.tile([P, 6], F32)
-        mv_p = keep.tile([P, 2], F32)
-        ve_p = keep.tile([P, 1], F32)
-        std_p = keep.tile([P, 1], F32)
-        rstd_p = keep.tile([P, 1], F32)
-        nmr_p = keep.tile([P, 1], F32)
-        z_p = keep.tile([P, D], F32)
-        pn_planes = keep.tile([P, T, P], BF16)
-        pn_g = keep.tile([P, P, T], BF16, align_bytes=64)
-        pn_c = keep.tile([P, P], U32, align_bytes=64)
-        pn_s = keep.tile([P, P], U8, align_bytes=64)
-        p0b = keep.tile([P, T, P], F32)
-        w_g = [keep.tile([P, D, T], BF16, name="wg%d" % h, align_bytes=64) for h in range(2)]
-        w_c = [keep.tile([P, D], U32, name="wc%d" % h, align_bytes=64) for h in range(2)]
-        w_s = [keep.tile([P, D], U8, name="ws%d" % h, align_bytes=64) for h in range(2)]
-        shared = keep.tile([P, B, P // B, T], F32)
-        st_c = keep.tile([P, T, 6], F32)
-        mv_c = keep.tile([P, T, 2], F32)
-        ve_c = keep.tile([P, T], F32)
-        std_c = keep.tile([P, T], F32)
-        rstd_c = keep.tile([P, T], F32)
-        negm_c = keep.tile([P, T], F32)
-        nmr_c = keep.tile([P, T], F32)
-        z_c = [keep.tile([P, D], F32, name="zc%d" % a) for a in range(T)]
-        col_planes = keep.tile([P, T, D], BF16)
-        col_g = keep.tile([P, D, T], BF16, align_bytes=64)
-        col_c = keep.tile([P, D], U32, align_bytes=64)
-        col_s = keep.tile([P, D], U8, align_bytes=64)
-        pv_g = [keep.tile([P, CH * P * 2], F32, name="pvg%d" % c, align_bytes=64) for c in range(NCH)]
-        pv_c = keep.tile([P, B * P], U32, align_bytes=64)
-        pv_s = keep.tile([P, B * P], U8, align_bytes=64)
-        x_g = [keep.tile([P, CH, P, T], BF16, name="xg%d" % c, align_bytes=64) for c in range(NCH)]
-        x_c = keep.tile([P, B * P], U32, align_bytes=64)
-        x_s = keep.tile([P, B * P], U8, align_bytes=64)
-        o_sb = [keep.tile([P, CH, D], F32, name="o%d" % c) for c in range(NCH)]
+        def vector_column(v, t):
+            return vectors[:, PACK * v + t : PACK * v + t + 1]
 
-        def s_ms():
-            nc.vector.memset(vec_rows[:], 0.0)
-            nc.vector.memset(one_t[:], 1.0)
-
-        def s_warm():
-            nc.scalar.activation(out=warm[:], in_=one_t[:], func=ACT.Sqrt)
-
-        def s_vec():
-            for v, vec in enumerate((ln_prompt_w, ln_prompt_b, b_imp, ln_col_w, ln_col_b)):
-                nc.sync.dma_start(out=vec_rows[T * v : T * v + T, :], in_=vec.rearrange("(t c) -> t c", c=P))
-
-        def s_ec():
-            nc.sync.dma_start(out=ec[:], in_=emb_column.rearrange("(a q) d -> q a d", q=P))
-
-        def s_w2():
-            nc.sync.dma_start(
-                out=w_raw[1][:].rearrange("q (u e) c -> q u (e c)", u=2),
-                in_=w_imp[D : 2 * D, :].rearrange("(u q e) c -> q u (e c)", u=2, e=2),
+        def regroup(engine, grouped, planes, cols):
+            copy_bits(
+                engine,
+                grouped[:, cols, :].rearrange("p (c i) t -> p c t i", i=RUN),
+                planes[:, :, cols].rearrange("p t (c i) -> p c t i", i=RUN),
             )
 
-        def s_pv(c):
-            nc.sync.dma_start(out=prev_sb[c][:], in_=pv_view[:, CH * c : CH * c + CH, :])
+        def quantise(words, scales, values):
+            nc.vector.quantize_mx(out=words.bitcast(FP8X4), scales=scales, in_=values)
 
-        def s_tvec():
-            live["vt"] = ps_tr.tile([P, P], BF16, tag="tr", name="vt_ps")
-            nc.tensor.transpose(live["vt"][:], vec_rows[:], ident_b[:])
-
-        def s_agp():
-            nc.vector.bn_aggr(out=mv_p[:], in_=st_p[:])
-            nc.vector.tensor_scalar_add(out=ve_p[:], in0=mv_p[:, 1:2], scalar1=EPS)
-
-        def s_rcp():
-            nc.vector.reciprocal(out=rstd_p[:], in_=std_p[:])
-            nc.vector.scalar_tensor_tensor(
-                out=nmr_p[:], in0=mv_p[:, 0:1], scalar=-1.0, in1=rstd_p[:], op0=ALU.mult, op1=ALU.mult
-            )
-
-        def s_zp():
-            if eng_of("zp") == "S":
-                nc.scalar.activation(out=z_p[:], in_=p0[:], func=ACT.Identity, scale=rstd_p[:], bias=nmr_p[:])
-            else:
-                nc.vector.tensor_scalar(
-                    out=z_p[:], in0=p0[:], scalar1=mv_p[:, 0:1], scalar2=rstd_p[:], op0=ALU.subtract, op1=ALU.mult
-                )
-
-        def s_tzp():
-            live["zp"] = ps_tr.tile([P, T, P], F32, tag="tr", name="zp_ps")
-            for t in range(T):
-                nc.tensor.transpose(live["zp"][:, t, :], z_p[:, t * P : (t + 1) * P], ident_f[:])
-
-        def s_pnact():
-            for t in range(T):
-                affine("pnact", pn_planes[:, t, :], live["zp"][:, t, :], vec_t[:, t : t + 1], vec_t[:, T + t : T + t + 1])
-
-        def s_tp0():
-            live["p0t"] = ps_tr.tile([P, T, P], BF16, tag="tr", name="p0t_ps")
-            for t in range(T):
-                nc.tensor.transpose(live["p0t"][:, t, :], p0[:, t * P : (t + 1) * P], ident_b[:])
-
-        def s_p0b():
-            if eng_of("p0b") == "S":
-                for t in range(T):
-                    nc.scalar.activation(
-                        out=p0b[:, t, :],
-                        in_=live["p0t"][:, t, :],
-                        func=ACT.Identity,
-                        bias=vec_t[:, 2 * T + t : 2 * T + t + 1],
-                        scale=1.0,
-                    )
-            else:
-                nc.vector.tensor_tensor(
-                    out=p0b[:],
-                    in0=live["p0t"][:],
-                    in1=vec_t[:, 2 * T : 3 * T].unsqueeze(2).to_broadcast([P, T, P]),
-                    op=ALU.add,
-                )
-
-        def regroup(name, grouped, planes, part, parts):
-            w = D // parts
-            cs = slice(part * w, (part + 1) * w)
-            move(
-                name,
-                grouped[:, cs, :].rearrange("p (c i) t -> p c t i", i=4),
-                planes[:, :, cs].rearrange("p t (c i) -> p c t i", i=4),
-            )
-
-        def quant(codes, scales, src):
-            nc.vector.quantize_mx(out=codes.bitcast(FP8X4), scales=scales, in_=src)
-
-        def mx(dst, lc, ls, rc, rs):
+        def matmul_mx(dst, l_words, l_scales, r_words, r_scales):
             nc.tensor.matmul_mx(
-                out=dst, lhsT=lc.bitcast(FP8X4), lhsT_scale=ls, rhs=rc.bitcast(FP8X4), rhs_scale=rs, start=True, stop=True
+                out=dst,
+                lhsT=l_words.bitcast(FP8X4),
+                lhsT_scale=l_scales,
+                rhs=r_words.bitcast(FP8X4),
+                rhs_scale=r_scales,
+                start=True,
+                stop=True,
             )
 
-        def s_mfp():
-            live["fp"] = ps_s1.tile([P, T, P], F32, tag="s1", name="fp_ps")
-            for t in range(T):
-                ts = slice(t * P, (t + 1) * P)
-                mx(live["fp"][:, t, :], w_c[0][:, ts], w_s[0][:, ts], pn_c[:], pn_s[:])
+        def span(i, width=P):
+            return slice(i * width, (i + 1) * width)
 
-        def s_shared():
+        def clear(engine):
+            nc.vector.memset(vector_rows[:], 0.0)
+            nc.vector.memset(one[:], 1.0)
+
+        def load_vectors(engine):
+            for v, vec in enumerate((ln_prompt_w, ln_prompt_b, b_imp, ln_col_w, ln_col_b)):
+                nc.sync.dma_start(out=vector_rows[PACK * v : PACK * (v + 1), :], in_=vec.rearrange("(t c) -> t c", c=P))
+
+        def load_w1(engine):
+            nc.sync.dma_start(
+                out=w_raw[1][:].rearrange("p (u e) c -> p u (e c)", u=2),
+                in_=w_imp[D : 2 * D, :].rearrange("(u p e) c -> p u (e c)", u=2, e=2),
+            )
+
+        step("clear", (VECTOR,), clear)
+        step(
+            "sqrt_table",
+            (SCALAR,),
+            lambda engine: nc.scalar.activation(out=sqrt_of_one[:], in_=one[:], func=ACT.Sqrt),
+        )
+        step("identity_f32", (GPSIMD,), lambda engine: make_identity(nc, identity_f32[:]))
+        step("identity_bf16", (GPSIMD,), lambda engine: make_identity(nc, identity_bf16[:]))
+        step("load_prompt", (SYNC,), lambda engine: nc.sync.dma_start(out=prompt[:], in_=emb_prompt))
+        step("load_vectors", (SYNC,), load_vectors)
+        step(
+            "load_column",
+            (SYNC,),
+            lambda engine: nc.sync.dma_start(out=emb_col[:], in_=emb_column.rearrange("(a q) d -> q a d", q=P)),
+        )
+        step(
+            "load_w0",
+            (SYNC,),
+            lambda engine: nc.sync.dma_start(out=w_raw[0][:], in_=w_imp[0:D, :].rearrange("(t p) c -> p t c", p=P)),
+        )
+        step("load_w1", (SYNC,), load_w1)
+        for c in range(PAIRS):
+            step(
+                "load_prev%d" % c,
+                (SYNC,),
+                lambda engine, c=c: nc.sync.dma_start(out=prev[c][:], in_=prev_rows[:, span(c, PAIR), :]),
+            )
+
+        def t_vectors(engine):
+            banks["vectors"] = ps_t.tile([P, P], BF16, tag="t", name="vectors_ps")
+            nc.tensor.transpose(banks["vectors"][:], vector_rows[:], identity_bf16[:])
+
+        step("T_vectors", (TENSOR,), t_vectors)
+        step(
+            "vectors",
+            (VECTOR,),
+            lambda engine: nc.vector.tensor_copy(out=vectors[:], in_=banks["vectors"][:, 0 : N_VECTORS * PACK]),
+        )
+
+        def p_var(engine):
+            nc.vector.bn_aggr(out=p_mean_var[:], in_=p_stats[:])
+            nc.vector.tensor_scalar_add(out=p_var_eps[:], in0=p_mean_var[:, 1:2], scalar1=EPS)
+
+        def p_rstd_step(engine):
+            nc.vector.reciprocal(out=p_rstd[:], in_=p_std[:])
+            nc.vector.scalar_tensor_tensor(
+                out=p_shift[:], in0=p_mean_var[:, 0:1], scalar=-1.0, in1=p_rstd[:], op0=ALU.mult, op1=ALU.mult
+            )
+
+        def t_p_norm(engine):
+            banks["p_norm"] = ps_t.tile([P, PACK, P], F32, tag="t", name="p_norm_ps")
+            for t in range(PACK):
+                nc.tensor.transpose(banks["p_norm"][:, t, :], p_norm[:, span(t)], identity_f32[:])
+
+        def p_gain(engine):
+            for t in range(PACK):
+                gain_and_bias(
+                    engine,
+                    pn_planes[:, t, :],
+                    banks["p_norm"][:, t, :],
+                    vector_column(LN_PROMPT_W, t),
+                    vector_column(LN_PROMPT_B, t),
+                )
+
+        step("p_stats", (VECTOR,), lambda engine: nc.vector.bn_stats(out=p_stats[:], in_=prompt[:]))
+        step("p_var", (VECTOR,), p_var)
+        step("p_std", (SCALAR,), lambda engine: nc.scalar.activation(out=p_std[:], in_=p_var_eps[:], func=ACT.Sqrt))
+        step("p_rstd", (VECTOR,), p_rstd_step)
+        step(
+            "p_norm",
+            (SCALAR,),
+            lambda engine: nc.scalar.activation(
+                out=p_norm[:], in_=prompt[:], func=ACT.Identity, scale=p_rstd[:], bias=p_shift[:]
+            ),
+        )
+        step("T_p_norm", (TENSOR,), t_p_norm)
+        step("p_gain", (SCALAR,), p_gain)
+        step(
+            "p_group",
+            (SCALAR,),
+            lambda engine: copy_bits(engine, pn_grouped[:], pn_planes[:].rearrange("p t r -> p r t")),
+        )
+        step(
+            "p_quant",
+            (VECTOR,),
+            lambda engine: quantise(pn_words[:], pn_scales[:], pn_grouped[:].rearrange("p r t -> p (r t)")),
+        )
+
+        def t_prompt(engine):
+            banks["prompt"] = ps_t.tile([P, PACK, P], BF16, tag="t", name="prompt_ps")
+            for t in range(PACK):
+                nc.tensor.transpose(banks["prompt"][:, t, :], prompt[:, span(t)], identity_bf16[:])
+
+        def p_bias(engine):
+            for t in range(PACK):
+                nc.scalar.activation(
+                    out=prompt_bias[:, t, :],
+                    in_=banks["prompt"][:, t, :],
+                    func=ACT.Identity,
+                    bias=vector_column(B_IMP, t),
+                    scale=1.0,
+                )
+
+        step("T_prompt", (TENSOR,), t_prompt)
+        step("p_bias", (SCALAR,), p_bias)
+
+        for h in range(2):
+            for i in range(QUARTERS):
+                step(
+                    "w%d_group%d" % (h, i),
+                    (VECTOR, SCALAR, GPSIMD),
+                    lambda engine, h=h, i=i: regroup(engine, w_grouped[h], w_raw[h], span(i, D // QUARTERS)),
+                )
+            step(
+                "w%d_quant" % h,
+                (VECTOR,),
+                lambda engine, h=h: quantise(
+                    w_words[h][:], w_scales[h][:], w_grouped[h][:].rearrange("p c t -> p (c t)")
+                ),
+            )
+
+        def mm_prompt(engine):
+            banks["from_prompt"] = ps_x.tile([P, PACK, P], F32, tag="x", name="from_prompt_ps")
+            for t in range(PACK):
+                matmul_mx(
+                    banks["from_prompt"][:, t, :], w_words[0][:, span(t)], w_scales[0][:, span(t)], pn_words[:], pn_scales[:]
+                )
+
+        def shared_step(engine):
             nc.vector.tensor_tensor(
                 out=shared[:].rearrange("p j i t -> p i j t"),
-                in0=live["fp"][:].rearrange("p t (i j) -> p i j t", j=B),
-                in1=p0b[:].rearrange("p t (i j) -> p i j t", j=B),
+                in0=banks["from_prompt"][:].rearrange("p t (i j) -> p i j t", j=TILES),
+                in1=prompt_bias[:].rearrange("p t (i j) -> p i j t", j=TILES),
                 op=ALU.add,
             )
 
-        def s_bnc(a):
-            nc.vector.bn_stats(out=st_c[:, a, :], in_=ec[:, a, :])
-            nc.vector.bn_aggr(out=mv_c[:, a, :], in_=st_c[:, a, :])
+        step("mm_prompt", (TENSOR,), mm_prompt)
+        step("shared", (VECTOR,), shared_step)
 
-        def s_vecc(h):
-            hs = slice(2 * h, 2 * h + 2)
-            nc.vector.tensor_scalar_add(out=ve_c[:, hs], in0=mv_c[:, hs, 1], scalar1=EPS)
-            nc.vector.tensor_scalar_mul(out=negm_c[:, hs], in0=mv_c[:, hs, 0], scalar1=-1.0)
+        def c_stats_step(engine, a):
+            nc.vector.bn_stats(out=c_stats[:, a, :], in_=emb_col[:, a, :])
+            nc.vector.bn_aggr(out=c_mean_var[:, a, :], in_=c_stats[:, a, :])
 
-        def s_sqc(h):
-            hs = slice(2 * h, 2 * h + 2)
-            nc.scalar.activation(out=std_c[:, hs], in_=ve_c[:, hs], func=ACT.Sqrt)
+        def c_var(engine, h):
+            nc.vector.tensor_scalar_add(out=c_var_eps[:, span(h, 2)], in0=c_mean_var[:, span(h, 2), 1], scalar1=EPS)
+            nc.vector.tensor_scalar_mul(out=c_neg_mean[:, span(h, 2)], in0=c_mean_var[:, span(h, 2), 0], scalar1=-1.0)
 
-        def s_rcc(h):
-            hs = slice(2 * h, 2 * h + 2)
-            nc.vector.reciprocal(out=rstd_c[:, hs], in_=std_c[:, hs])
-            nc.vector.tensor_tensor(out=nmr_c[:, hs], in0=negm_c[:, hs], in1=rstd_c[:, hs], op=ALU.mult)
+        def c_rstd_step(engine, h):
+            nc.vector.reciprocal(out=c_rstd[:, span(h, 2)], in_=c_std[:, span(h, 2)])
+            nc.vector.tensor_tensor(
+                out=c_shift[:, span(h, 2)], in0=c_neg_mean[:, span(h, 2)], in1=c_rstd[:, span(h, 2)], op=ALU.mult
+            )
 
-        def s_qc(h):
-            cs = slice(h * D // 2, (h + 1) * D // 2)
-            quant(col_c[:, cs], col_s[:, cs], col_g[:, cs, :].rearrange("p c t -> p (c t)"))
-
-        def s_zc(a):
-            e = eng_of("zc%d" % a)
-            if e == "S":
+        def c_norm_step(engine, a):
+            one_col = slice(a, a + 1)
+            if engine == SCALAR:
                 nc.scalar.activation(
-                    out=z_c[a][:], in_=ec[:, a, :], func=ACT.Identity, scale=rstd_c[:, a : a + 1], bias=nmr_c[:, a : a + 1]
+                    out=c_norm[a][:],
+                    in_=emb_col[:, a, :],
+                    func=ACT.Identity,
+                    scale=c_rstd[:, one_col],
+                    bias=c_shift[:, one_col],
                 )
             else:
-                (nc.vector if e == "V" else nc.gpsimd).tensor_scalar(
-                    out=z_c[a][:],
-                    in0=ec[:, a, :],
-                    scalar1=negm_c[:, a : a + 1],
-                    scalar2=rstd_c[:, a : a + 1],
+                nc.gpsimd.tensor_scalar(
+                    out=c_norm[a][:],
+                    in0=emb_col[:, a, :],
+                    scalar1=c_neg_mean[:, one_col],
+                    scalar2=c_rstd[:, one_col],
                     op0=ALU.add,
                     op1=ALU.mult,
                 )
 
-        def s_tzc(i):
-            h, tp = i // 2, i % 2
-            live["ct%d" % i] = ps_s2.tile([P, 2, 2, P], F32, tag="s2", name="ct_ps%d" % i)
+        def t_c_norm(engine, i):
+            h, s = i // 2, i % 2
+            banks["c_norm%d" % i] = ps_o.tile([P, 2, 2, P], F32, tag="o", name="c_norm_ps%d" % i)
             for tt in range(2):
-                t = 2 * tp + tt
                 for aa in range(2):
-                    nc.tensor.transpose(live["ct%d" % i][:, tt, aa, :], z_c[2 * h + aa][:, t * P : (t + 1) * P], ident_f[:])
+                    nc.tensor.transpose(
+                        banks["c_norm%d" % i][:, tt, aa, :], c_norm[2 * h + aa][:, span(2 * s + tt)], identity_f32[:]
+                    )
 
-        def s_cact(i):
-            h, tp = i // 2, i % 2
+        def c_gain(engine, i):
+            h, s = i // 2, i % 2
             for tt in range(2):
-                t = 2 * tp + tt
-                affine(
-                    "cact%d" % i,
-                    col_planes[:, t, h * D // 2 : (h + 1) * D // 2],
-                    live["ct%d" % i][:, tt].rearrange("k a q -> k (a q)"),
-                    vec_t[:, 3 * T + t : 3 * T + t + 1],
-                    vec_t[:, 4 * T + t : 4 * T + t + 1],
+                t = 2 * s + tt
+                gain_and_bias(
+                    engine,
+                    col_planes[:, t, span(h, HALF)],
+                    banks["c_norm%d" % i][:, tt].rearrange("p a q -> p (a q)"),
+                    vector_column(LN_COL_W, t),
+                    vector_column(LN_COL_B, t),
                 )
 
-        def s_tr(c):
-            words = prev_sb[c][:].rearrange("p s d -> p (s d)").bitcast(F32)
-            live["tr%d" % c] = ps_tr.tile([P, CH, 2, P], F32, tag="tr", name="tr_ps%d" % c)
-            for s in range(CH):
-                for u in range(2):
-                    lo = s * (D // 2) + u * P
-                    nc.tensor.transpose(live["tr%d" % c][:, s, u, :], words[:, lo : lo + P], ident_f[:])
-
-        def s_cp(c):
-            move(
-                "CP%d" % c,
-                pv_g[c][:].rearrange("p (s r u) -> p s r u", s=CH, u=2),
-                live["tr%d" % c][:].rearrange("p s u r -> p s r u"),
+        for a in range(PACK):
+            step("c_stats%d" % a, (VECTOR,), lambda engine, a=a: c_stats_step(engine, a))
+            step("c_norm%d" % a, (SCALAR, GPSIMD), lambda engine, a=a: c_norm_step(engine, a))
+            step("T_c_norm%d" % a, (TENSOR,), lambda engine, a=a: t_c_norm(engine, a))
+            step("c_gain%d" % a, (SCALAR, VECTOR), lambda engine, a=a: c_gain(engine, a))
+        for h in range(HALVES):
+            step("c_var%d" % h, (VECTOR,), lambda engine, h=h: c_var(engine, h))
+            step(
+                "c_std%d" % h,
+                (SCALAR,),
+                lambda engine, h=h: nc.scalar.activation(
+                    out=c_std[:, span(h, 2)], in_=c_var_eps[:, span(h, 2)], func=ACT.Sqrt
+                ),
+            )
+            step("c_rstd%d" % h, (VECTOR,), lambda engine, h=h: c_rstd_step(engine, h))
+            step(
+                "c_group%d" % h,
+                (SCALAR, GPSIMD),
+                lambda engine, h=h: regroup(engine, col_grouped, col_planes, span(h, HALF)),
+            )
+            step(
+                "c_quant%d" % h,
+                (VECTOR,),
+                lambda engine, h=h: quantise(
+                    col_words[:, span(h, HALF)],
+                    col_scales[:, span(h, HALF)],
+                    col_grouped[:, span(h, HALF), :].rearrange("p c t -> p (c t)"),
+                ),
             )
 
-        def s_qp(c):
-            cs = slice(c * CH * P, (c + 1) * CH * P)
-            quant(pv_c[:, cs], pv_s[:, cs], pv_g[c][:].bitcast(BF16))
+        def t_prev(engine, c):
+            words = prev[c][:].rearrange("p s d -> p (s d)").bitcast(F32)
+            banks["prev%d" % c] = ps_t.tile([P, PAIR, 2, P], F32, tag="t", name="prev_ps%d" % c)
+            for s in range(PAIR):
+                for u in range(2):
+                    nc.tensor.transpose(banks["prev%d" % c][:, s, u, :], words[:, span(2 * s + u)], identity_f32[:])
 
-        def s_m1(n):
-            live["s1_%d" % n] = ps_s1.tile([P, T, P], F32, tag="s1", name="s1_ps%d" % n)
-            ns = slice(n * P, (n + 1) * P)
-            for t in range(T):
-                ts = slice(t * P, (t + 1) * P)
-                mx(live["s1_%d" % n][:, t, :], w_c[1][:, ts], w_s[1][:, ts], pv_c[:, ns], pv_s[:, ns])
+        def prev_copy(engine, c):
+            copy_bits(
+                engine,
+                prev_grouped[c][:].rearrange("p (s r u) -> p s r u", s=PAIR, u=2),
+                banks["prev%d" % c][:].rearrange("p s u r -> p s r u"),
+            )
 
-        def s_ad(n):
+        def mm_x(engine, j):
+            banks["x%d" % j] = ps_x.tile([P, PACK, P], F32, tag="x", name="x_ps%d" % j)
+            for t in range(PACK):
+                matmul_mx(
+                    banks["x%d" % j][:, t, :],
+                    w_words[1][:, span(t)],
+                    w_scales[1][:, span(t)],
+                    prev_words[:, span(j)],
+                    prev_scales[:, span(j)],
+                )
+
+        def x_add(engine, j):
             nc.vector.tensor_tensor(
-                out=x_g[n // CH][:, n % CH].rearrange("p (m i) t -> p m i t", m=B),
-                in0=live["s1_%d" % n][:].rearrange("p t (m i) -> p m i t", m=B),
-                in1=shared[:, n].unsqueeze(1).to_broadcast([P, B, P // B, T]),
+                out=x_grouped[j // PAIR][:, j % PAIR].rearrange("p (m i) t -> p m i t", i=PER_TILE),
+                in0=banks["x%d" % j][:].rearrange("p t (m i) -> p m i t", i=PER_TILE),
+                in1=shared[:, j].unsqueeze(1).to_broadcast([P, P // PER_TILE, PER_TILE, PACK]),
                 op=ALU.add,
             )
 
-        def s_qx(c):
-            cs = slice(c * CH * P, (c + 1) * CH * P)
-            quant(x_c[:, cs], x_s[:, cs], x_g[c][:].rearrange("p s r t -> p (s r t)"))
-
-        def s_m2(n):
-            if n % 5 < 3:
-                live["s2_%d" % n] = ps_s2.tile([P, D], F32, tag="s2", name="s2_ps%d" % n)
+        def mm_out(engine, j):
+            if j % (O_BANKS + T_BANKS) < O_BANKS:
+                banks["out%d" % j] = ps_o.tile([P, D], F32, tag="o", name="out_ps%d" % j)
             else:
-                live["s2_%d" % n] = ps_tr.tile([P, D], F32, tag="tr", name="s2_ps%d" % n)
-            ns = slice(n * P, (n + 1) * P)
-            mx(live["s2_%d" % n][:], x_c[:, ns], x_s[:, ns], col_c[:], col_s[:])
+                banks["out%d" % j] = ps_t.tile([P, D], F32, tag="t", name="out_ps%d" % j)
+            matmul_mx(banks["out%d" % j][:], x_words[:, span(j)], x_scales[:, span(j)], col_words[:], col_scales[:])
 
-        def s_st(c):
-            nc.sync.dma_start(out=out_view[:, CH * c : CH * c + CH, :], in_=o_sb[c][:])
+        for c in range(PAIRS):
+            step("T_prev%d" % c, (TENSOR,), lambda engine, c=c: t_prev(engine, c))
+            step("prev_copy%d" % c, (SCALAR,), lambda engine, c=c: prev_copy(engine, c))
+            step(
+                "prev_quant%d" % c,
+                (VECTOR,),
+                lambda engine, c=c: quantise(
+                    prev_words[:, span(c, PAIR * P)],
+                    prev_scales[:, span(c, PAIR * P)],
+                    prev_grouped[c][:].bitcast(BF16),
+                ),
+            )
+        for j in range(TILES):
+            step("mm_x%d" % j, (TENSOR,), lambda engine, j=j: mm_x(engine, j))
+            step("x_add%d" % j, (VECTOR,), lambda engine, j=j: x_add(engine, j))
+            step("mm_out%d" % j, (TENSOR,), lambda engine, j=j: mm_out(engine, j))
+            step(
+                "out_copy%d" % j,
+                (SCALAR, VECTOR),
+                lambda engine, j=j: copy_bits(engine, result[j // PAIR][:, j % PAIR, :], banks["out%d" % j][:]),
+            )
+        for c in range(PAIRS - 1):
+            step(
+                "x_quant%d" % c,
+                (VECTOR,),
+                lambda engine, c=c: quantise(
+                    x_words[:, span(c, PAIR * P)],
+                    x_scales[:, span(c, PAIR * P)],
+                    x_grouped[c][:].rearrange("p s r t -> p (s r t)"),
+                ),
+            )
+            step(
+                "store%d" % c,
+                (SYNC,),
+                lambda engine, c=c: nc.sync.dma_start(out=out_rows[:, span(c, PAIR), :], in_=result[c][:]),
+            )
+        for j in range(TILES - PAIR, TILES):
+            step(
+                "x_quant_tile%d" % j,
+                (VECTOR,),
+                lambda engine, j=j: quantise(
+                    x_words[:, span(j)],
+                    x_scales[:, span(j)],
+                    x_grouped[j // PAIR][:, j % PAIR].rearrange("p r t -> p (r t)"),
+                ),
+            )
+            step(
+                "store_tile%d" % j,
+                (SYNC,),
+                lambda engine, j=j: nc.sync.dma_start(out=out_rows[:, j, :], in_=result[j // PAIR][:, j % PAIR, :]),
+            )
 
-        def s_sth(n):
-            nc.sync.dma_start(out=out_view[:, n, :], in_=o_sb[n // CH][:, n % CH, :])
-
-        def s_qxh(n):
-            ns = slice(n * P, (n + 1) * P)
-            quant(x_c[:, ns], x_s[:, ns], x_g[n // CH][:, n % CH].rearrange("p r t -> p (r t)"))
-
-        steps["ms"] = s_ms
-        steps["warm"] = s_warm
-        steps["idb"] = lambda: make_identity(nc, ident_b[:])
-        steps["idf"] = lambda: make_identity(nc, ident_f[:])
-        steps["vec"] = s_vec
-        steps["p0"] = lambda: nc.sync.dma_start(out=p0[:], in_=emb_prompt)
-        steps["ec"] = s_ec
-        steps["w1"] = lambda: nc.sync.dma_start(out=w_raw[0][:], in_=w_imp[0:D, :].rearrange("(t p) e -> p t e", p=P))
-        steps["w2"] = s_w2
-        steps["Tvec"] = s_tvec
-        steps["vec_t"] = lambda: nc.vector.tensor_copy(out=vec_t[:], in_=live["vt"][:, 0 : 5 * T])
-        steps["bnp"] = lambda: nc.vector.bn_stats(out=st_p[:], in_=p0[:])
-        steps["agp"] = s_agp
-        steps["sqp"] = lambda: nc.scalar.activation(out=std_p[:], in_=ve_p[:], func=ACT.Sqrt)
-        steps["rcp"] = s_rcp
-        steps["zp"] = s_zp
-        steps["Tzp"] = s_tzp
-        steps["pnact"] = s_pnact
-        steps["pnrg"] = lambda: move("pnrg", pn_g[:], pn_planes[:].rearrange("p t r -> p r t"))
-        steps["Qpn"] = lambda: quant(pn_c[:], pn_s[:], pn_g[:].rearrange("p r t -> p (r t)"))
-        steps["Tp0"] = s_tp0
-        steps["p0b"] = s_p0b
-        steps["Mfp"] = s_mfp
-        steps["shared"] = s_shared
-        for h in range(2):
-            steps["vecc%d" % h] = lambda h=h: s_vecc(h)
-            steps["sqc%d" % h] = lambda h=h: s_sqc(h)
-            steps["rcc%d" % h] = lambda h=h: s_rcc(h)
-            steps["Qc%d" % h] = lambda h=h: s_qc(h)
-        for h, parts in ((0, WP1), (1, WP2)):
-            for i in range(parts):
-                steps["wrg%d_%d" % (h + 1, i)] = lambda h=h, i=i, parts=parts: regroup(
-                    "wrg%d_%d" % (h + 1, i), w_g[h], w_raw[h], i, parts
-                )
-            steps["QW%d" % (h + 1)] = lambda h=h: quant(w_c[h][:], w_s[h][:], w_g[h][:].rearrange("p c t -> p (c t)"))
-        for i in range(CPARTS):
-            steps["crg%d" % i] = lambda i=i: regroup("crg%d" % i, col_g, col_planes, i, CPARTS)
-        for a in range(T):
-            steps["bnc%d" % a] = lambda a=a: s_bnc(a)
-            steps["zc%d" % a] = lambda a=a: s_zc(a)
-            steps["Tzc%d" % a] = lambda a=a: s_tzc(a)
-            steps["cact%d" % a] = lambda a=a: s_cact(a)
-        for c in range(NCH):
-            steps["pv%d" % c] = lambda c=c: s_pv(c)
-            steps["TR%d" % c] = lambda c=c: s_tr(c)
-            steps["CP%d" % c] = lambda c=c: s_cp(c)
-            steps["QP%d" % c] = lambda c=c: s_qp(c)
-        for c in range(NCH - 1):
-            steps["QX%d" % c] = lambda c=c: s_qx(c)
-            steps["ST%d" % c] = lambda c=c: s_st(c)
-        for n in (B - 2, B - 1):
-            steps["QXh%d" % n] = lambda n=n: s_qxh(n)
-            steps["STh%d" % n] = lambda n=n: s_sth(n)
-        for n in range(B):
-            steps["M1_%d" % n] = lambda n=n: s_m1(n)
-            steps["AD%d" % n] = lambda n=n: s_ad(n)
-            steps["M2_%d" % n] = lambda n=n: s_m2(n)
-            steps["CO%d" % n] = lambda n=n: move("CO%d" % n, o_sb[n // CH][:, n % CH, :], live["s2_%d" % n][:])
-
-        assert len(ORDER) == len(steps)
-        for name in ORDER:
-            steps[name]()
+        assert sorted([name for row in SCHEDULE for name in row if name]) == sorted(steps)
+        for row in SCHEDULE:
+            for engine, name in zip(ENGINES, row):
+                if name:
+                    engines, emit = steps[name]
+                    assert engine in engines, name
+                    emit(engine)

@@ -46,61 +46,61 @@ ENGINES = (SYNC, GPSIMD, TENSOR, VECTOR, SCALAR)
 
 SCHEDULE = (
     ("load_prompt",    "identity_f32",    "",             "clear",           "sqrt_table"),
-    ("load_vectors",   "identity_bf16",   "T_vectors",    "p_stats",         ""),
-    ("load_column",    "",                "T_prompt",     "p_var",           "p_std"),
-    ("load_w0",        "w0_group1",       "",             "vectors",         "p_bias"),
-    ("load_w1",        "w1_group1",       "",             "p_rstd",          "p_norm"),
-    ("load_prev0",     "",                "T_p_norm",     "c_stats0",        "w0_group2"),
-    ("load_prev1",     "",                "T_prev0",      "c_stats1",        "w0_group0"),
-    ("load_prev2",     "",                "",             "c_var0",          "p_gain"),
-    ("load_prev3",     "",                "T_prev1",      "c_stats2",        "p_group"),
-    ("load_prev4",     "",                "",             "w0_group3",       "w1_group3"),
-    ("load_prev5",     "",                "",             "c_stats3",        "prev_copy0"),
-    ("load_prev6",     "",                "T_prev2",      "c_var1",          "c_std0"),
-    ("load_prev7",     "",                "",             "w0_quant",        "prev_copy1"),
-    ("",               "",                "",             "w1_group2",       "c_std1"),
-    ("",               "",                "",             "w1_group0",       ""),
+    ("load_column",    "identity_bf16",   "",             "p_stats",         ""),
+    ("load_vectors",   "",                "T_vectors",    "p_var",           "p_std"),
+    ("load_w0",        "w0_group3",       "T_prompt",     "c_stats0",        "w0_group2"),
+    ("load_w1",        "w1_group2",       "",             "p_rstd",          "w0_group1"),
+    ("load_prev0",     "w1_group1",       "",             "vectors",         "w1_group0"),
+    ("load_prev1",     "",                "",             "p_norm",          ""),
+    ("load_prev2",     "",                "T_p_norm",     "w0_group0",       "p_gain"),
+    ("load_prev4",     "",                "",             "p_bias",          "w1_group3"),
+    ("load_prev3",     "",                "T_prev0",      "c_stats2",        "prev_copy0"),
+    ("load_prev5",     "",                "T_prev1",      "c_stats3",        ""),
+    ("load_prev7",     "",                "T_prev2",      "c_stats1",        ""),
+    ("load_prev6",     "",                "",             "c_var",           "c_std"),
+    ("",               "",                "",             "p_group",         "prev_copy1"),
+    ("",               "",                "T_prev3",      "w0_quant",        ""),
     ("",               "",                "",             "p_quant",         ""),
     ("",               "",                "mm_prompt",    "w1_quant",        ""),
-    ("",               "",                "",             "prev_quant0",     ""),
-    ("",               "",                "mm_x0",        "c_rstd0",         "c_norm0"),
-    ("",               "c_norm1",         "mm_x1",        "prev_quant1",     "prev_copy2"),
-    ("",               "",                "T_prev3",      "c_rstd1",         "c_norm2"),
-    ("",               "c_norm3",         "T_c_norm0",    "shared",          "prev_copy3"),
-    ("",               "",                "T_c_norm1",    "x_add0",          "c_gain0"),
-    ("",               "",                "mm_x2",        "x_add1",          "c_gain1"),
-    ("",               "c_group0",        "mm_x3",        "prev_quant2",     ""),
-    ("",               "",                "T_c_norm2",    "x_quant0",        ""),
-    ("",               "",                "T_prev4",      "prev_quant3",     "prev_copy4"),
-    ("",               "",                "T_c_norm3",    "x_add2",          "c_gain3"),
-    ("",               "",                "mm_x4",        "c_gain2",         "c_group1"),
-    ("",               "",                "mm_x5",        "x_add3",          ""),
-    ("",               "",                "T_prev5",      "x_add4",          "prev_copy5"),
-    ("",               "",                "mm_x6",        "prev_quant4",     ""),
-    ("",               "",                "mm_x7",        "c_quant0",        ""),
-    ("",               "",                "T_prev6",      "x_add5",          "prev_copy6"),
-    ("",               "",                "T_prev7",      "c_quant1",        "prev_copy7"),
-    ("",               "",                "mm_out0",      "x_quant1",        "out_copy0"),
+    ("",               "",                "",             "c_rstd",          "c_norm3"),
+    ("",               "c_norm0",         "",             "prev_quant0",     "c_norm2"),
+    ("",               "c_norm1",         "mm_x0",        "prev_copy2",      "prev_copy3"),
+    ("",               "",                "mm_x1",        "shared",          ""),
+    ("",               "",                "T_prev4",      "prev_quant1",     "prev_copy4"),
+    ("",               "",                "T_c_norm0",    "x_add0",          "c_gain0"),
+    ("",               "",                "T_prev5",      "prev_quant3",     "prev_copy5"),
+    ("",               "",                "T_c_norm1",    "x_add1",          "c_gain1"),
+    ("",               "",                "mm_x3",        "prev_quant2",     ""),
+    ("",               "",                "T_c_norm3",    "prev_quant4",     ""),
+    ("",               "",                "T_c_norm2",    "x_add3",          "c_gain2"),
+    ("",               "",                "T_prev6",      "c_gain3",         "c_group1"),
+    ("",               "c_group0",        "mm_x5",        "prev_quant5",     ""),
+    ("",               "",                "mm_x2",        "x_add5",          ""),
+    ("",               "",                "mm_x4",        "x_add2",          ""),
+    ("",               "",                "T_prev7",      "x_add4",          "prev_copy7"),
+    ("",               "",                "mm_x6",        "x_quant0",        "prev_copy6"),
+    ("",               "",                "mm_x7",        "c_quant",         ""),
+    ("",               "",                "mm_x11",       "x_quant1",        ""),
+    ("",               "",                "mm_out0",      "x_add6",          "out_copy0"),
     ("",               "",                "mm_out1",      "x_quant2",        "out_copy1"),
-    ("store0",         "",                "mm_out2",      "x_add6",          "out_copy2"),
-    ("",               "",                "mm_x8",        "x_add7",          ""),
-    ("",               "",                "mm_out3",      "prev_quant5",     "out_copy3"),
-    ("store1",         "",                "mm_x9",        "x_quant3",        ""),
-    ("",               "",                "mm_x10",       "prev_quant6",     ""),
-    ("",               "",                "mm_out4",      "x_add8",          "out_copy4"),
+    ("store0",         "",                "mm_x9",        "x_add7",          ""),
+    ("",               "",                "mm_out2",      "x_add11",         "out_copy2"),
+    ("",               "",                "mm_out3",      "x_quant3",        "out_copy3"),
+    ("store1",         "",                "mm_x8",        "prev_quant6",     ""),
     ("",               "",                "mm_out5",      "x_add9",          "out_copy5"),
-    ("store2",         "",                "mm_x11",       "x_add10",         ""),
-    ("",               "",                "mm_out6",      "x_quant4",        "out_copy6"),
-    ("",               "",                "mm_out7",      "x_add11",         "out_copy7"),
-    ("store3",         "",                "mm_x12",       "x_quant5",        ""),
-    ("",               "",                "mm_x13",       "prev_quant7",     ""),
-    ("",               "",                "mm_out8",      "x_add12",         "out_copy8"),
-    ("",               "",                "mm_out9",      "x_add13",         "out_copy9"),
-    ("store4",         "",                "mm_out10",     "x_quant6",        "out_copy10"),
-    ("",               "",                "mm_x14",       "x_add14",         ""),
+    ("",               "",                "mm_x10",       "x_add8",          ""),
+    ("",               "",                "mm_out4",      "x_quant4",        "out_copy4"),
+    ("store2",         "",                "mm_x12",       "prev_quant7",     ""),
+    ("",               "",                "mm_out7",      "x_add10",         "out_copy7"),
+    ("",               "",                "mm_out6",      "x_quant5",        "out_copy6"),
+    ("store3",         "",                "mm_out8",      "x_add12",         "out_copy8"),
+    ("",               "",                "mm_x13",       "x_add13",         ""),
+    ("",               "",                "mm_out9",      "x_quant6",        "out_copy9"),
+    ("store4",         "",                "mm_x14",       "x_add14",         ""),
+    ("",               "",                "mm_out10",     "x_quant_tile14",  "out_copy10"),
     ("",               "",                "mm_x15",       "x_add15",         ""),
-    ("",               "",                "mm_out11",     "x_quant_tile14",  "out_copy11"),
-    ("store5",         "",                "mm_out12",     "x_quant_tile15",  "out_copy12"),
+    ("",               "",                "mm_out11",     "x_quant_tile15",  "out_copy11"),
+    ("store5",         "",                "mm_out12",     "",                "out_copy12"),
     ("",               "",                "mm_out13",     "out_copy13",      ""),
     ("store6",         "",                "mm_out14",     "",                "out_copy14"),
     ("store_tile14",   "",                "mm_out15",     "out_copy15",      ""),
@@ -135,7 +135,6 @@ def tile_tromptcell_pa_kernel(
         p_var_eps = keep.tile([P, 1], F32)
         p_std = keep.tile([P, 1], F32)
         p_rstd = keep.tile([P, 1], F32)
-        p_shift = keep.tile([P, 1], F32)
         p_norm = keep.tile([P, D], F32)
         pn_planes = keep.tile([P, PACK, P], BF16)
         pn_grouped = keep.tile([P, P, PACK], BF16, align_bytes=64)
@@ -248,7 +247,9 @@ def tile_tromptcell_pa_kernel(
         step(
             "load_column",
             (SYNC,),
-            lambda engine: nc.sync.dma_start(out=emb_col[:], in_=emb_column.rearrange("(a q) d -> q a d", q=P)),
+            lambda engine: nc.sync.dma_start(
+                out=emb_col[:].rearrange("q a d -> q (a d)"), in_=emb_column.rearrange("(q a) d -> q (a d)", a=PACK)
+            ),
         )
         step(
             "load_w0",
@@ -278,12 +279,6 @@ def tile_tromptcell_pa_kernel(
             nc.vector.bn_aggr(out=p_mean_var[:], in_=p_stats[:])
             nc.vector.tensor_scalar_add(out=p_var_eps[:], in0=p_mean_var[:, 1:2], scalar1=EPS)
 
-        def p_rstd_step(engine):
-            nc.vector.reciprocal(out=p_rstd[:], in_=p_std[:])
-            nc.vector.scalar_tensor_tensor(
-                out=p_shift[:], in0=p_mean_var[:, 0:1], scalar=-1.0, in1=p_rstd[:], op0=ALU.mult, op1=ALU.mult
-            )
-
         def t_p_norm(engine):
             banks["p_norm"] = ps_t.tile([P, PACK, P], F32, tag="t", name="p_norm_ps")
             for t in range(PACK):
@@ -302,19 +297,24 @@ def tile_tromptcell_pa_kernel(
         step("p_stats", (VECTOR,), lambda engine: nc.vector.bn_stats(out=p_stats[:], in_=prompt[:]))
         step("p_var", (VECTOR,), p_var)
         step("p_std", (SCALAR,), lambda engine: nc.scalar.activation(out=p_std[:], in_=p_var_eps[:], func=ACT.Sqrt))
-        step("p_rstd", (VECTOR,), p_rstd_step)
+        step("p_rstd", (VECTOR,), lambda engine: nc.vector.reciprocal(out=p_rstd[:], in_=p_std[:]))
         step(
             "p_norm",
-            (SCALAR,),
-            lambda engine: nc.scalar.activation(
-                out=p_norm[:], in_=prompt[:], func=ACT.Identity, scale=p_rstd[:], bias=p_shift[:]
+            (VECTOR,),
+            lambda engine: nc.vector.tensor_scalar(
+                out=p_norm[:],
+                in0=prompt[:],
+                scalar1=p_mean_var[:, 0:1],
+                scalar2=p_rstd[:],
+                op0=ALU.subtract,
+                op1=ALU.mult,
             ),
         )
         step("T_p_norm", (TENSOR,), t_p_norm)
         step("p_gain", (SCALAR,), p_gain)
         step(
             "p_group",
-            (SCALAR,),
+            (VECTOR,),
             lambda engine: copy_bits(engine, pn_grouped[:], pn_planes[:].rearrange("p t r -> p r t")),
         )
         step(
@@ -329,17 +329,15 @@ def tile_tromptcell_pa_kernel(
                 nc.tensor.transpose(banks["prompt"][:, t, :], prompt[:, span(t)], identity_bf16[:])
 
         def p_bias(engine):
-            for t in range(PACK):
-                nc.scalar.activation(
-                    out=prompt_bias[:, t, :],
-                    in_=banks["prompt"][:, t, :],
-                    func=ACT.Identity,
-                    bias=vector_column(B_IMP, t),
-                    scale=1.0,
-                )
+            nc.vector.tensor_tensor(
+                out=prompt_bias[:],
+                in0=banks["prompt"][:],
+                in1=vectors[:, span(B_IMP, PACK)].unsqueeze(2).to_broadcast([P, PACK, P]),
+                op=ALU.add,
+            )
 
         step("T_prompt", (TENSOR,), t_prompt)
-        step("p_bias", (SCALAR,), p_bias)
+        step("p_bias", (VECTOR,), p_bias)
 
         for h in range(2):
             for i in range(QUARTERS):
@@ -360,7 +358,11 @@ def tile_tromptcell_pa_kernel(
             banks["from_prompt"] = ps_x.tile([P, PACK, P], F32, tag="x", name="from_prompt_ps")
             for t in range(PACK):
                 matmul_mx(
-                    banks["from_prompt"][:, t, :], w_words[0][:, span(t)], w_scales[0][:, span(t)], pn_words[:], pn_scales[:]
+                    banks["from_prompt"][:, t, :],
+                    w_words[0][:, span(t)],
+                    w_scales[0][:, span(t)],
+                    pn_words[:],
+                    pn_scales[:],
                 )
 
         def shared_step(engine):
@@ -378,15 +380,13 @@ def tile_tromptcell_pa_kernel(
             nc.vector.bn_stats(out=c_stats[:, a, :], in_=emb_col[:, a, :])
             nc.vector.bn_aggr(out=c_mean_var[:, a, :], in_=c_stats[:, a, :])
 
-        def c_var(engine, h):
-            nc.vector.tensor_scalar_add(out=c_var_eps[:, span(h, 2)], in0=c_mean_var[:, span(h, 2), 1], scalar1=EPS)
-            nc.vector.tensor_scalar_mul(out=c_neg_mean[:, span(h, 2)], in0=c_mean_var[:, span(h, 2), 0], scalar1=-1.0)
+        def c_var(engine):
+            nc.vector.tensor_scalar_add(out=c_var_eps[:], in0=c_mean_var[:, :, 1], scalar1=EPS)
+            nc.vector.tensor_scalar_mul(out=c_neg_mean[:], in0=c_mean_var[:, :, 0], scalar1=-1.0)
 
-        def c_rstd_step(engine, h):
-            nc.vector.reciprocal(out=c_rstd[:, span(h, 2)], in_=c_std[:, span(h, 2)])
-            nc.vector.tensor_tensor(
-                out=c_shift[:, span(h, 2)], in0=c_neg_mean[:, span(h, 2)], in1=c_rstd[:, span(h, 2)], op=ALU.mult
-            )
+        def c_rstd_step(engine):
+            nc.vector.reciprocal(out=c_rstd[:], in_=c_std[:])
+            nc.vector.tensor_tensor(out=c_shift[:], in0=c_neg_mean[:], in1=c_rstd[:], op=ALU.mult)
 
         def c_norm_step(engine, a):
             one_col = slice(a, a + 1)
@@ -408,56 +408,40 @@ def tile_tromptcell_pa_kernel(
                     op1=ALU.mult,
                 )
 
-        def t_c_norm(engine, i):
-            h, s = i // 2, i % 2
-            banks["c_norm%d" % i] = ps_o.tile([P, 2, 2, P], F32, tag="o", name="c_norm_ps%d" % i)
-            for tt in range(2):
-                for aa in range(2):
-                    nc.tensor.transpose(
-                        banks["c_norm%d" % i][:, tt, aa, :], c_norm[2 * h + aa][:, span(2 * s + tt)], identity_f32[:]
-                    )
+        def t_c_norm(engine, t):
+            banks["c_norm%d" % t] = ps_o.tile([P, PACK, P], F32, tag="o", name="c_norm_ps%d" % t)
+            for a in range(PACK):
+                nc.tensor.transpose(banks["c_norm%d" % t][:, a, :], c_norm[a][:, span(t)], identity_f32[:])
 
-        def c_gain(engine, i):
-            h, s = i // 2, i % 2
-            for tt in range(2):
-                t = 2 * s + tt
-                gain_and_bias(
-                    engine,
-                    col_planes[:, t, span(h, HALF)],
-                    banks["c_norm%d" % i][:, tt].rearrange("p a q -> p (a q)"),
-                    vector_column(LN_COL_W, t),
-                    vector_column(LN_COL_B, t),
-                )
+        def c_gain(engine, t):
+            gain_and_bias(
+                engine,
+                col_planes[:, t, :].rearrange("p (q a) -> p q a", a=PACK),
+                banks["c_norm%d" % t][:].rearrange("p a q -> p q a"),
+                vector_column(LN_COL_W, t),
+                vector_column(LN_COL_B, t),
+            )
 
         for a in range(PACK):
             step("c_stats%d" % a, (VECTOR,), lambda engine, a=a: c_stats_step(engine, a))
             step("c_norm%d" % a, (SCALAR, GPSIMD), lambda engine, a=a: c_norm_step(engine, a))
-            step("T_c_norm%d" % a, (TENSOR,), lambda engine, a=a: t_c_norm(engine, a))
-            step("c_gain%d" % a, (SCALAR, VECTOR), lambda engine, a=a: c_gain(engine, a))
+        for t in range(PACK):
+            step("T_c_norm%d" % t, (TENSOR,), lambda engine, t=t: t_c_norm(engine, t))
+            step("c_gain%d" % t, (SCALAR, VECTOR), lambda engine, t=t: c_gain(engine, t))
+        step("c_var", (VECTOR,), c_var)
+        step("c_std", (SCALAR,), lambda engine: nc.scalar.activation(out=c_std[:], in_=c_var_eps[:], func=ACT.Sqrt))
+        step("c_rstd", (VECTOR,), c_rstd_step)
         for h in range(HALVES):
-            step("c_var%d" % h, (VECTOR,), lambda engine, h=h: c_var(engine, h))
-            step(
-                "c_std%d" % h,
-                (SCALAR,),
-                lambda engine, h=h: nc.scalar.activation(
-                    out=c_std[:, span(h, 2)], in_=c_var_eps[:, span(h, 2)], func=ACT.Sqrt
-                ),
-            )
-            step("c_rstd%d" % h, (VECTOR,), lambda engine, h=h: c_rstd_step(engine, h))
             step(
                 "c_group%d" % h,
                 (SCALAR, GPSIMD),
                 lambda engine, h=h: regroup(engine, col_grouped, col_planes, span(h, HALF)),
             )
-            step(
-                "c_quant%d" % h,
-                (VECTOR,),
-                lambda engine, h=h: quantise(
-                    col_words[:, span(h, HALF)],
-                    col_scales[:, span(h, HALF)],
-                    col_grouped[:, span(h, HALF), :].rearrange("p c t -> p (c t)"),
-                ),
-            )
+        step(
+            "c_quant",
+            (VECTOR,),
+            lambda engine: quantise(col_words[:], col_scales[:], col_grouped[:].rearrange("p c t -> p (c t)")),
+        )
 
         def t_prev(engine, c):
             words = prev[c][:].rearrange("p s d -> p (s d)").bitcast(F32)
@@ -493,15 +477,12 @@ def tile_tromptcell_pa_kernel(
             )
 
         def mm_out(engine, j):
-            if j % (O_BANKS + T_BANKS) < O_BANKS:
-                banks["out%d" % j] = ps_o.tile([P, D], F32, tag="o", name="out_ps%d" % j)
-            else:
-                banks["out%d" % j] = ps_t.tile([P, D], F32, tag="t", name="out_ps%d" % j)
+            banks["out%d" % j] = ps_o.tile([P, D], F32, tag="o", name="out_ps%d" % j)
             matmul_mx(banks["out%d" % j][:], x_words[:, span(j)], x_scales[:, span(j)], col_words[:], col_scales[:])
 
         for c in range(PAIRS):
             step("T_prev%d" % c, (TENSOR,), lambda engine, c=c: t_prev(engine, c))
-            step("prev_copy%d" % c, (SCALAR,), lambda engine, c=c: prev_copy(engine, c))
+            step("prev_copy%d" % c, (SCALAR, VECTOR), lambda engine, c=c: prev_copy(engine, c))
             step(
                 "prev_quant%d" % c,
                 (VECTOR,),

@@ -45,65 +45,64 @@ SCALAR = "scalar"
 ENGINES = (SYNC, GPSIMD, TENSOR, VECTOR, SCALAR)
 
 SCHEDULE = (
-    ("load_prompt",    "identity_f32",    "",             "clear",           "sqrt_table"),
-    ("load_column",    "identity_bf16",   "",             "p_stats",         ""),
+    ("load_prompt",    "identity_bf16",   "",             "clear",           "sqrt_table"),
+    ("load_column",    "identity_f32",    "",             "p_stats",         ""),
     ("load_vectors",   "",                "T_vectors",    "p_var",           "p_std"),
-    ("load_w0",        "w0_group3",       "T_prompt",     "c_stats0",        "w0_group2"),
-    ("load_w1",        "w1_group2",       "",             "p_rstd",          "w0_group1"),
-    ("load_prev0",     "w1_group1",       "",             "vectors",         "w1_group0"),
+    ("load_w0",        "w0_group0",       "T_prompt",     "c_stats0",        "w0_group1"),
+    ("load_w1",        "w1_group2",       "",             "p_rstd",          "w0_group2"),
+    ("load_prev0",     "w1_group1",       "",             "vectors",         "w0_group3"),
     ("load_prev1",     "",                "",             "p_norm",          ""),
-    ("load_prev2",     "",                "T_p_norm",     "w0_group0",       "p_gain"),
-    ("load_prev4",     "",                "",             "p_bias",          "w1_group3"),
-    ("load_prev3",     "",                "T_prev0",      "c_stats2",        "prev_copy0"),
-    ("load_prev5",     "",                "T_prev1",      "c_stats3",        ""),
-    ("load_prev7",     "",                "T_prev2",      "c_stats1",        ""),
+    ("load_prev4",     "",                "T_p_norm",     "p_bias",          "p_gain"),
+    ("load_prev3",     "",                "T_prev0",      "c_stats1",        "w1_group3"),
+    ("load_prev2",     "",                "T_prev1",      "c_stats2",        "w1_group0"),
+    ("load_prev7",     "",                "",             "c_stats3",        ""),
     ("load_prev6",     "",                "",             "c_var",           "c_std"),
-    ("",               "",                "",             "p_group",         "prev_copy1"),
-    ("",               "",                "T_prev3",      "w0_quant",        ""),
+    ("load_prev5",     "",                "",             "p_group",         "prev_copy0"),
+    ("",               "",                "T_prev3",      "w0_quant",        "prev_copy1"),
     ("",               "",                "",             "p_quant",         ""),
-    ("",               "",                "mm_prompt",    "w1_quant",        ""),
-    ("",               "",                "",             "c_rstd",          "c_norm3"),
-    ("",               "c_norm0",         "",             "prev_quant0",     "c_norm2"),
-    ("",               "c_norm1",         "mm_x0",        "prev_copy2",      "prev_copy3"),
+    ("",               "",                "mm_prompt",    "c_rstd",          "c_norm2"),
+    ("",               "c_norm0",         "T_prev2",      "w1_quant",        "prev_copy3"),
+    ("",               "c_norm1",         "",             "prev_quant0",     "c_norm3"),
+    ("",               "",                "mm_x0",        "prev_quant1",     "prev_copy2"),
     ("",               "",                "mm_x1",        "shared",          ""),
-    ("",               "",                "T_prev4",      "prev_quant1",     "prev_copy4"),
-    ("",               "",                "T_c_norm0",    "x_add0",          "c_gain0"),
-    ("",               "",                "T_prev5",      "prev_quant3",     "prev_copy5"),
-    ("",               "",                "T_c_norm1",    "x_add1",          "c_gain1"),
-    ("",               "",                "mm_x3",        "prev_quant2",     ""),
+    ("",               "",                "T_prev4",      "x_add0",          "prev_copy4"),
+    ("",               "",                "T_c_norm0",    "x_add1",          "c_gain0"),
+    ("",               "",                "T_c_norm1",    "prev_quant2",     ""),
+    ("",               "",                "T_prev5",      "x_quant0",        "prev_copy5"),
+    ("",               "",                "mm_x3",        "prev_quant3",     "c_gain1"),
     ("",               "",                "T_c_norm3",    "prev_quant4",     ""),
     ("",               "",                "T_c_norm2",    "x_add3",          "c_gain2"),
-    ("",               "",                "T_prev6",      "c_gain3",         "c_group1"),
-    ("",               "c_group0",        "mm_x5",        "prev_quant5",     ""),
-    ("",               "",                "mm_x2",        "x_add5",          ""),
-    ("",               "",                "mm_x4",        "x_add2",          ""),
-    ("",               "",                "T_prev7",      "x_add4",          "prev_copy7"),
-    ("",               "",                "mm_x6",        "x_quant0",        "prev_copy6"),
-    ("",               "",                "mm_x7",        "c_quant",         ""),
-    ("",               "",                "mm_x11",       "x_quant1",        ""),
+    ("",               "",                "T_prev6",      "c_gain3",         "prev_copy6"),
+    ("",               "c_group0",        "mm_x2",        "prev_quant5",     "c_group1"),
+    ("",               "",                "mm_x5",        "x_add2",          ""),
+    ("",               "",                "T_prev7",      "x_add5",          "prev_copy7"),
+    ("",               "",                "mm_x4",        "x_add4",          ""),
+    ("",               "",                "mm_x6",        "prev_quant6",     ""),
+    ("",               "",                "mm_x11",       "c_quant",         ""),
+    ("",               "",                "mm_x7",        "x_quant1",        ""),
     ("",               "",                "mm_out0",      "x_add6",          "out_copy0"),
     ("",               "",                "mm_out1",      "x_quant2",        "out_copy1"),
-    ("store0",         "",                "mm_x9",        "x_add7",          ""),
-    ("",               "",                "mm_out2",      "x_add11",         "out_copy2"),
+    ("store0",         "",                "mm_out2",      "x_add11",         "out_copy2"),
+    ("",               "",                "mm_x8",        "x_add7",          ""),
+    ("",               "",                "mm_x9",        "x_add8",          ""),
     ("",               "",                "mm_out3",      "x_quant3",        "out_copy3"),
-    ("store1",         "",                "mm_x8",        "prev_quant6",     ""),
-    ("",               "",                "mm_out5",      "x_add9",          "out_copy5"),
-    ("",               "",                "mm_x10",       "x_add8",          ""),
+    ("store1",         "",                "mm_x10",       "x_add9",          ""),
+    ("",               "",                "mm_out5",      "x_add10",         "out_copy5"),
     ("",               "",                "mm_out4",      "x_quant4",        "out_copy4"),
-    ("store2",         "",                "mm_x12",       "prev_quant7",     ""),
-    ("",               "",                "mm_out7",      "x_add10",         "out_copy7"),
-    ("",               "",                "mm_out6",      "x_quant5",        "out_copy6"),
-    ("store3",         "",                "mm_out8",      "x_add12",         "out_copy8"),
-    ("",               "",                "mm_x13",       "x_add13",         ""),
-    ("",               "",                "mm_out9",      "x_quant6",        "out_copy9"),
+    ("store2",         "",                "mm_out7",      "prev_quant7",     "out_copy7"),
+    ("",               "",                "mm_x12",       "x_quant5",        ""),
+    ("",               "",                "mm_out6",      "x_add12",         "out_copy6"),
+    ("store3",         "",                "mm_x13",       "x_add13",         ""),
+    ("",               "",                "mm_out8",      "x_quant6",        "out_copy8"),
+    ("",               "",                "mm_out9",      "",                "out_copy9"),
     ("store4",         "",                "mm_x14",       "x_add14",         ""),
-    ("",               "",                "mm_out10",     "x_quant_tile14",  "out_copy10"),
+    ("",               "",                "mm_out10",     "",                "out_copy10"),
     ("",               "",                "mm_x15",       "x_add15",         ""),
-    ("",               "",                "mm_out11",     "x_quant_tile15",  "out_copy11"),
-    ("store5",         "",                "mm_out12",     "",                "out_copy12"),
+    ("",               "",                "mm_out11",     "x_quant_tile14",  "out_copy11"),
+    ("store5",         "",                "mm_out12",     "x_quant_tile15",  "out_copy12"),
     ("",               "",                "mm_out13",     "out_copy13",      ""),
     ("store6",         "",                "mm_out14",     "",                "out_copy14"),
-    ("store_tile14",   "",                "mm_out15",     "out_copy15",      ""),
+    ("store_tile14",   "",                "mm_out15",     "",                "out_copy15"),
     ("store_tile15",   "",                "",             "",                ""),
 )
 

@@ -17,6 +17,7 @@ PACK = 4
 TILES = 16
 PAIR = 2
 PAIRS = TILES // PAIR
+TILE_STORES = TILES - 2 * PAIR
 PER_TILE = P // TILES
 QUARTERS = 4
 HALVES = 2
@@ -101,8 +102,9 @@ SCHEDULE = (
     ("",               "",                "mm_out11",     "x_quant_tile14",  "out_copy11"),
     ("store5",         "",                "mm_out12",     "x_quant_tile15",  "out_copy12"),
     ("",               "",                "mm_out13",     "out_copy13",      ""),
-    ("store6",         "",                "mm_out14",     "",                "out_copy14"),
-    ("store_tile14",   "",                "mm_out15",     "",                "out_copy15"),
+    ("store_tile12",   "",                "mm_out14",     "",                "out_copy14"),
+    ("store_tile13",   "",                "mm_out15",     "out_copy15",      ""),
+    ("store_tile14",   "",                "",             "",                ""),
     ("store_tile15",   "",                "",             "",                ""),
 )
 
@@ -510,6 +512,7 @@ def tile_tromptcell_pa_kernel(
                     x_grouped[c][:].rearrange("p s r t -> p (s r t)"),
                 ),
             )
+        for c in range(TILE_STORES // PAIR):
             step(
                 "store%d" % c,
                 (SYNC,),
@@ -525,6 +528,7 @@ def tile_tromptcell_pa_kernel(
                     x_grouped[j // PAIR][:, j % PAIR].rearrange("p r t -> p (r t)"),
                 ),
             )
+        for j in range(TILE_STORES, TILES):
             step(
                 "store_tile%d" % j,
                 (SYNC,),

@@ -46,26 +46,30 @@ SCALAR = "scalar"
 ENGINES = (SYNC, GPSIMD, TENSOR, VECTOR, SCALAR)
 
 SCHEDULE = (
-    ("load_prompt",    "identity_bf16",   "",             "clear",           "sqrt_table"),
-    ("load_column",    "identity_f32",    "",             "p_stats",         ""),
-    ("load_vectors",   "",                "T_vectors",    "p_var",           "p_std"),
-    ("load_w0",        "w0_group0",       "T_prompt",     "c_stats0",        "w0_group1"),
-    ("load_w1",        "w1_group2",       "",             "p_rstd",          "w0_group2"),
-    ("load_prev0",     "w1_group1",       "",             "vectors",         "w0_group3"),
-    ("load_prev1",     "",                "",             "p_norm",          ""),
-    ("load_prev4",     "",                "T_p_norm",     "p_bias",          "p_gain"),
+    ("load_prompt",    "identity_bf16",   "",             "clear",           "rstd_table"),
+    ("load_column0",   "identity_f32",    "",             "p_stats",         "p_rstd"),
+    ("load_vectors",   "",                "T_vectors",    "c_stats0",        "vectors"),
+    ("load_w0",        "w0_group1",       "T_prompt",     "",                "w0_group2"),
+    ("load_column1",   "w0_group0",       "",             "",                "w0_group3"),
+    ("load_w1",        "w1_group2",       "",             "",                ""),
+    ("load_prev0",     "w1_group1",       "",             "p_norm",          ""),
+    ("load_prev1",     "",                "T_p_norm",     "c_aggr0",         "p_gain"),
+    ("load_prev4",     "",                "",             "p_bias",          ""),
     ("load_prev3",     "",                "T_prev0",      "c_stats1",        "w1_group3"),
     ("load_prev2",     "",                "T_prev1",      "c_stats2",        "w1_group0"),
+    ("",               "",                "",             "c_aggr1",         ""),
     ("load_prev7",     "",                "",             "c_stats3",        ""),
-    ("load_prev6",     "",                "",             "c_var",           "c_std"),
+    ("",               "",                "",             "c_aggr2",         ""),
+    ("load_prev6",     "",                "",             "c_aggr3",         "c_rstd"),
     ("load_prev5",     "",                "",             "p_group",         "prev_copy0"),
     ("",               "",                "T_prev3",      "w0_quant",        "prev_copy1"),
     ("",               "",                "",             "p_quant",         ""),
-    ("",               "",                "mm_prompt",    "c_rstd",          "c_norm2"),
+    ("",               "c_shift",         "mm_prompt",    "",                "c_norm2"),
     ("",               "c_norm0",         "T_prev2",      "w1_quant",        "prev_copy3"),
     ("",               "c_norm1",         "",             "prev_quant0",     "c_norm3"),
-    ("",               "",                "mm_x0",        "prev_quant1",     "prev_copy2"),
-    ("",               "",                "mm_x1",        "shared",          ""),
+    ("",               "",                "mm_x0",        "shared",          "prev_copy2"),
+    ("",               "",                "",             "prev_quant1",     ""),
+    ("",               "",                "mm_x1",        "",                ""),
     ("",               "",                "T_prev4",      "x_add0",          "prev_copy4"),
     ("",               "",                "T_c_norm0",    "x_add1",          "c_gain0"),
     ("",               "",                "T_c_norm1",    "prev_quant2",     ""),
@@ -82,9 +86,9 @@ SCHEDULE = (
     ("",               "",                "mm_x11",       "c_quant",         ""),
     ("",               "",                "mm_x7",        "x_quant1",        ""),
     ("",               "",                "mm_out0",      "x_add6",          "out_copy0"),
-    ("",               "",                "mm_out1",      "x_quant2",        "out_copy1"),
-    ("store0",         "",                "mm_out2",      "x_add11",         "out_copy2"),
-    ("",               "",                "mm_x8",        "x_add7",          ""),
+    ("",               "",                "mm_out1",      "x_add11",         "out_copy1"),
+    ("store0",         "",                "mm_out2",      "x_add7",          "out_copy2"),
+    ("",               "",                "mm_x8",        "x_quant2",        ""),
     ("",               "",                "mm_x9",        "x_add8",          ""),
     ("",               "",                "mm_out3",      "x_quant3",        "out_copy3"),
     ("store1",         "",                "mm_x10",       "x_add9",          ""),
@@ -94,10 +98,10 @@ SCHEDULE = (
     ("",               "",                "mm_x12",       "x_quant5",        ""),
     ("",               "",                "mm_out6",      "x_add12",         "out_copy6"),
     ("store3",         "",                "mm_x13",       "x_add13",         ""),
-    ("",               "",                "mm_out8",      "x_quant6",        "out_copy8"),
+    ("",               "",                "mm_out8",      "",                "out_copy8"),
     ("",               "",                "mm_out9",      "",                "out_copy9"),
     ("store4",         "",                "mm_x14",       "x_add14",         ""),
-    ("",               "",                "mm_out10",     "",                "out_copy10"),
+    ("",               "",                "mm_out10",     "x_quant6",        "out_copy10"),
     ("",               "",                "mm_x15",       "x_add15",         ""),
     ("",               "",                "mm_out11",     "x_quant_tile14",  "out_copy11"),
     ("store5",         "",                "mm_out12",     "x_quant_tile15",  "out_copy12"),
@@ -125,16 +129,15 @@ def tile_tromptcell_pa_kernel(
 
         vector_rows = keep.tile([P, P], BF16)
         vectors = keep.tile([P, N_VECTORS * PACK], F32)
-        one = keep.tile([P, 1], F32)
-        sqrt_of_one = keep.tile([P, 1], F32)
+        zero = keep.tile([P, 1], F32)
+        eps = keep.tile([P, 1], F32)
+        table_loaded = keep.tile([P, 1], F32)
         identity_bf16 = keep.tile([P, P], BF16)
         identity_f32 = keep.tile([P, P], F32)
 
         prompt = keep.tile([P, D], BF16)
         p_stats = keep.tile([P, BN_STATS], F32)
         p_mean_var = keep.tile([P, BN_AGGR], F32)
-        p_var_eps = keep.tile([P, 1], F32)
-        p_std = keep.tile([P, 1], F32)
         p_rstd = keep.tile([P, 1], F32)
         p_norm = keep.tile([P, D], F32)
         pn_planes = keep.tile([P, PACK, P], BF16)
@@ -152,10 +155,8 @@ def tile_tromptcell_pa_kernel(
         emb_col = keep.tile([P, PACK, D], BF16)
         c_stats = keep.tile([P, PACK, BN_STATS], F32)
         c_mean_var = keep.tile([P, PACK, BN_AGGR], F32)
-        c_var_eps = keep.tile([P, PACK], F32)
-        c_std = keep.tile([P, PACK], F32)
         c_rstd = keep.tile([P, PACK], F32)
-        c_neg_mean = keep.tile([P, PACK], F32)
+        c_mean_rstd = keep.tile([P, PACK], F32)
         c_shift = keep.tile([P, PACK], F32)
         c_norm = [keep.tile([P, D], F32, name="c_norm%d" % a) for a in range(PACK)]
         col_planes = keep.tile([P, PACK, D], BF16)
@@ -194,6 +195,9 @@ def tile_tromptcell_pa_kernel(
             else:
                 nc.vector.tensor_scalar(out=dst, in0=src, scalar1=gain, scalar2=bias, op0=ALU.mult, op1=ALU.add)
 
+        def rstd(dst, variance):
+            nc.scalar.activation(out=dst, in_=variance, func=ACT.Abs_reciprocal_sqrt, bias=eps[:])
+
         def vector_column(v, t):
             return vectors[:, PACK * v + t : PACK * v + t + 1]
 
@@ -223,7 +227,8 @@ def tile_tromptcell_pa_kernel(
 
         def clear(engine):
             nc.vector.memset(vector_rows[:], 0.0)
-            nc.vector.memset(one[:], 1.0)
+            nc.vector.memset(zero[:], 0.0)
+            nc.vector.tensor_scalar_add(out=eps[:], in0=zero[:], scalar1=EPS)
 
         def load_vectors(engine):
             for v, vec in enumerate((ln_prompt_w, ln_prompt_b, b_imp, ln_col_w, ln_col_b)):
@@ -236,22 +241,20 @@ def tile_tromptcell_pa_kernel(
             )
 
         step("clear", (VECTOR,), clear)
-        step(
-            "sqrt_table",
-            (SCALAR,),
-            lambda engine: nc.scalar.activation(out=sqrt_of_one[:], in_=one[:], func=ACT.Sqrt),
-        )
+        step("rstd_table", (SCALAR,), lambda engine: rstd(table_loaded[:], eps[:]))
         step("identity_f32", (GPSIMD,), lambda engine: make_identity(nc, identity_f32[:]))
         step("identity_bf16", (GPSIMD,), lambda engine: make_identity(nc, identity_bf16[:]))
         step("load_prompt", (SYNC,), lambda engine: nc.sync.dma_start(out=prompt[:], in_=emb_prompt))
         step("load_vectors", (SYNC,), load_vectors)
-        step(
-            "load_column",
-            (SYNC,),
-            lambda engine: nc.sync.dma_start(
-                out=emb_col[:].rearrange("q a d -> q (a d)"), in_=emb_column.rearrange("(q a) d -> q (a d)", a=PACK)
-            ),
-        )
+        for h in range(2):
+            step(
+                "load_column%d" % h,
+                (SYNC,),
+                lambda engine, h=h: nc.sync.dma_start(
+                    out=emb_col[:, span(h, PACK // 2), :],
+                    in_=emb_column.rearrange("(q a) d -> q a d", a=PACK)[:, span(h, PACK // 2), :],
+                ),
+            )
         step(
             "load_w0",
             (SYNC,),
@@ -272,13 +275,13 @@ def tile_tromptcell_pa_kernel(
         step("T_vectors", (TENSOR,), t_vectors)
         step(
             "vectors",
-            (VECTOR,),
-            lambda engine: nc.vector.tensor_copy(out=vectors[:], in_=banks["vectors"][:, 0 : N_VECTORS * PACK]),
+            (SCALAR,),
+            lambda engine: copy_bits(engine, vectors[:], banks["vectors"][:, 0 : N_VECTORS * PACK]),
         )
 
-        def p_var(engine):
+        def p_stats_step(engine):
+            nc.vector.bn_stats(out=p_stats[:], in_=prompt[:])
             nc.vector.bn_aggr(out=p_mean_var[:], in_=p_stats[:])
-            nc.vector.tensor_scalar_add(out=p_var_eps[:], in0=p_mean_var[:, 1:2], scalar1=EPS)
 
         def t_p_norm(engine):
             banks["p_norm"] = ps_t.tile([P, PACK, P], F32, tag="t", name="p_norm_ps")
@@ -295,10 +298,8 @@ def tile_tromptcell_pa_kernel(
                     vector_column(LN_PROMPT_B, t),
                 )
 
-        step("p_stats", (VECTOR,), lambda engine: nc.vector.bn_stats(out=p_stats[:], in_=prompt[:]))
-        step("p_var", (VECTOR,), p_var)
-        step("p_std", (SCALAR,), lambda engine: nc.scalar.activation(out=p_std[:], in_=p_var_eps[:], func=ACT.Sqrt))
-        step("p_rstd", (VECTOR,), lambda engine: nc.vector.reciprocal(out=p_rstd[:], in_=p_std[:]))
+        step("p_stats", (VECTOR,), p_stats_step)
+        step("p_rstd", (SCALAR,), lambda engine: rstd(p_rstd[:], p_mean_var[:, 1:2]))
         step(
             "p_norm",
             (VECTOR,),
@@ -379,15 +380,15 @@ def tile_tromptcell_pa_kernel(
 
         def c_stats_step(engine, a):
             nc.vector.bn_stats(out=c_stats[:, a, :], in_=emb_col[:, a, :])
+
+        def c_aggr_step(engine, a):
             nc.vector.bn_aggr(out=c_mean_var[:, a, :], in_=c_stats[:, a, :])
 
-        def c_var(engine):
-            nc.vector.tensor_scalar_add(out=c_var_eps[:], in0=c_mean_var[:, :, 1], scalar1=EPS)
-            nc.vector.tensor_scalar_mul(out=c_neg_mean[:], in0=c_mean_var[:, :, 0], scalar1=-1.0)
-
-        def c_rstd_step(engine):
-            nc.vector.reciprocal(out=c_rstd[:], in_=c_std[:])
-            nc.vector.tensor_tensor(out=c_shift[:], in0=c_neg_mean[:], in1=c_rstd[:], op=ALU.mult)
+        def c_shift_step(engine):
+            nc.gpsimd.tensor_tensor(out=c_mean_rstd[:], in0=c_mean_var[:, :, 0], in1=c_rstd[:], op=ALU.mult)
+            nc.gpsimd.tensor_scalar(
+                out=c_shift[:], in0=c_mean_rstd[:], scalar1=-1.0, scalar2=0.0, op0=ALU.mult, op1=ALU.add
+            )
 
         def c_norm_step(engine, a):
             one_col = slice(a, a + 1)
@@ -403,10 +404,10 @@ def tile_tromptcell_pa_kernel(
                 nc.gpsimd.tensor_scalar(
                     out=c_norm[a][:],
                     in0=emb_col[:, a, :],
-                    scalar1=c_neg_mean[:, one_col],
-                    scalar2=c_rstd[:, one_col],
-                    op0=ALU.add,
-                    op1=ALU.mult,
+                    scalar1=c_rstd[:, one_col],
+                    scalar2=c_shift[:, one_col],
+                    op0=ALU.mult,
+                    op1=ALU.add,
                 )
 
         def t_c_norm(engine, t):
@@ -425,13 +426,13 @@ def tile_tromptcell_pa_kernel(
 
         for a in range(PACK):
             step("c_stats%d" % a, (VECTOR,), lambda engine, a=a: c_stats_step(engine, a))
+            step("c_aggr%d" % a, (VECTOR,), lambda engine, a=a: c_aggr_step(engine, a))
             step("c_norm%d" % a, (SCALAR, GPSIMD), lambda engine, a=a: c_norm_step(engine, a))
         for t in range(PACK):
             step("T_c_norm%d" % t, (TENSOR,), lambda engine, t=t: t_c_norm(engine, t))
             step("c_gain%d" % t, (SCALAR, VECTOR), lambda engine, t=t: c_gain(engine, t))
-        step("c_var", (VECTOR,), c_var)
-        step("c_std", (SCALAR,), lambda engine: nc.scalar.activation(out=c_std[:], in_=c_var_eps[:], func=ACT.Sqrt))
-        step("c_rstd", (VECTOR,), c_rstd_step)
+        step("c_rstd", (SCALAR,), lambda engine: rstd(c_rstd[:], c_mean_var[:, :, 1]))
+        step("c_shift", (GPSIMD,), c_shift_step)
         for h in range(HALVES):
             step(
                 "c_group%d" % h,

from contextlib import ExitStack

import concourse.mybir as mybir
from concourse.masks import make_identity

F32 = mybir.dt.float32
BF16 = mybir.dt.bfloat16
U32 = mybir.dt.uint32
U8 = mybir.dt.uint8
FP8X4 = mybir.dt.float8_e4m3fn_x4
ALU = mybir.AluOpType
ACT = mybir.ActivationFunctionType

P = 128
D = 512
PACK = 4
TILES = 16
PAIR = 2
PAIRS = TILES // PAIR
TILE_STORES = TILES - 2 * PAIR
PER_TILE = P // TILES
QUARTERS = 4
HALVES = 2
HALF = D // HALVES
EPS = 1e-5
N_VECTORS = 5
LN_PROMPT_W = 0
LN_PROMPT_B = 1
B_IMP = 2
LN_COL_W = 3
LN_COL_B = 4
BN_STATS = 6
BN_AGGR = 2
RUN = 4
T_BANKS = 2
X_BANKS = 3
O_BANKS = 3

FLOPS = 2 * P * D * D + 2 * 2 * TILES * P * D * D

SYNC = "sync"
GPSIMD = "gpsimd"
TENSOR = "tensor"
VECTOR = "vector"
SCALAR = "scalar"
ENGINES = (SYNC, GPSIMD, TENSOR, VECTOR, SCALAR)

SCHEDULE = (
    ("load_prompt",    "identity_bf16",   "",             "clear",           "rstd_table"),
    ("load_column0",   "identity_f32",    "",             "p_stats",         "p_rstd"),
    ("load_vectors",   "",                "T_vectors",    "c_stats0",        "vectors"),
    ("load_w0",        "w0_group1",       "T_prompt",     "",                "w0_group2"),
    ("load_column1",   "w0_group0",       "",             "",                "w0_group3"),
    ("load_w1",        "w1_group2",       "",             "",                ""),
    ("load_prev0",     "w1_group1",       "",             "p_norm",          ""),
    ("load_prev1",     "",                "T_p_norm",     "c_aggr0",         "p_gain"),
    ("load_prev4",     "",                "",             "p_bias",          ""),
    ("load_prev3",     "",                "T_prev0",      "c_stats1",        "w1_group3"),
    ("load_prev2",     "",                "T_prev1",      "c_stats2",        "w1_group0"),
    ("",               "",                "",             "c_aggr1",         ""),
    ("load_prev7",     "",                "",             "c_stats3",        ""),
    ("",               "",                "",             "c_aggr2",         ""),
    ("load_prev6",     "",                "",             "c_aggr3",         "c_rstd"),
    ("load_prev5",     "",                "",             "p_group",         "prev_copy0"),
    ("",               "",                "T_prev3",      "w0_quant",        "prev_copy1"),
    ("",               "",                "",             "p_quant",         ""),
    ("",               "c_shift",         "mm_prompt",    "",                "c_norm2"),
    ("",               "c_norm0",         "T_prev2",      "w1_quant",        "prev_copy3"),
    ("",               "c_norm1",         "",             "prev_quant0",     "c_norm3"),
    ("",               "",                "mm_x0",        "shared",          "prev_copy2"),
    ("",               "",                "",             "prev_quant1",     ""),
    ("",               "",                "mm_x1",        "",                ""),
    ("",               "",                "T_prev4",      "x_add0",          "prev_copy4"),
    ("",               "",                "T_c_norm0",    "x_add1",          "c_gain0"),
    ("",               "",                "T_c_norm1",    "prev_quant2",     ""),
    ("",               "",                "T_prev5",      "x_quant0",        "prev_copy5"),
    ("",               "",                "mm_x3",        "prev_quant3",     "c_gain1"),
    ("",               "",                "T_c_norm3",    "prev_quant4",     ""),
    ("",               "",                "T_c_norm2",    "x_add3",          "c_gain2"),
    ("",               "",                "T_prev6",      "c_gain3",         "prev_copy6"),
    ("",               "c_group0",        "mm_x2",        "prev_quant5",     "c_group1"),
    ("",               "",                "mm_x5",        "x_add2",          ""),
    ("",               "",                "T_prev7",      "x_add5",          "prev_copy7"),
    ("",               "",                "mm_x4",        "x_add4",          ""),
    ("",               "",                "mm_x6",        "prev_quant6",     ""),
    ("",               "",                "mm_x11",       "c_quant",         ""),
    ("",               "",                "mm_x7",        "x_quant1",        ""),
    ("",               "",                "mm_out0",      "x_add6",          "out_copy0"),
    ("",               "",                "mm_out1",      "x_add11",         "out_copy1"),
    ("store0",         "",                "mm_out2",      "x_add7",          "out_copy2"),
    ("",               "",                "mm_x8",        "x_quant2",        ""),
    ("",               "",                "mm_x9",        "x_add8",          ""),
    ("",               "",                "mm_out3",      "x_quant3",        "out_copy3"),
    ("store1",         "",                "mm_x10",       "x_add9",          ""),
    ("",               "",                "mm_out5",      "x_add10",         "out_copy5"),
    ("",               "",                "mm_out4",      "x_quant4",        "out_copy4"),
    ("store2",         "",                "mm_out7",      "prev_quant7",     "out_copy7"),
    ("",               "",                "mm_x12",       "x_quant5",        ""),
    ("",               "",                "mm_out6",      "x_add12",         "out_copy6"),
    ("store3",         "",                "mm_x13",       "x_add13",         ""),
    ("",               "",                "mm_out8",      "",                "out_copy8"),
    ("",               "",                "mm_out9",      "",                "out_copy9"),
    ("store4",         "",                "mm_x14",       "x_add14",         ""),
    ("",               "",                "mm_out10",     "x_quant6",        "out_copy10"),
    ("",               "",                "mm_x15",       "x_add15",         ""),
    ("",               "",                "mm_out11",     "x_quant_tile14",  "out_copy11"),
    ("store5",         "",                "mm_out12",     "x_quant_tile15",  "out_copy12"),
    ("",               "",                "mm_out13",     "out_copy13",      ""),
    ("store_tile12",   "",                "mm_out14",     "",                "out_copy14"),
    ("store_tile13",   "",                "mm_out15",     "out_copy15",      ""),
    ("store_tile14",   "",                "",             "",                ""),
    ("store_tile15",   "",                "",             "",                ""),
)


def tile_tromptcell_pa_kernel(
    tc, prev_cell_out, emb_prompt, ln_prompt_w, ln_prompt_b, w_imp, b_imp, emb_column, ln_col_w, ln_col_b, out
):
    nc = tc.nc
    prev_rows = prev_cell_out.flatten_outer_dims().rearrange("(q j) d -> q j d", j=TILES)
    out_rows = out.flatten_outer_dims().rearrange("(q j) c -> q j c", j=TILES)

    with ExitStack() as ctx:
        keep = ctx.enter_context(tc.tile_pool(name="keep", bufs=1))
        ps_t = ctx.enter_context(tc.psum_pool(name="ps_t", bufs=T_BANKS))
        ps_x = ctx.enter_context(tc.psum_pool(name="ps_x", bufs=X_BANKS))
        ps_o = ctx.enter_context(tc.psum_pool(name="ps_o", bufs=O_BANKS))
        ctx.enter_context(tc.manual_schedule())

        vector_rows = keep.tile([P, P], BF16)
        vectors = keep.tile([P, N_VECTORS * PACK], F32)
        zero = keep.tile([P, 1], F32)
        eps = keep.tile([P, 1], F32)
        table_loaded = keep.tile([P, 1], F32)
        identity_bf16 = keep.tile([P, P], BF16)
        identity_f32 = keep.tile([P, P], F32)

        prompt = keep.tile([P, D], BF16)
        p_stats = keep.tile([P, BN_STATS], F32)
        p_mean_var = keep.tile([P, BN_AGGR], F32)
        p_rstd = keep.tile([P, 1], F32)
        p_norm = keep.tile([P, D], F32)
        pn_planes = keep.tile([P, PACK, P], BF16)
        pn_grouped = keep.tile([P, P, PACK], BF16, align_bytes=64)
        pn_words = keep.tile([P, P], U32, align_bytes=64)
        pn_scales = keep.tile([P, P], U8, align_bytes=64)
        prompt_bias = keep.tile([P, PACK, P], F32)
        shared = keep.tile([P, TILES, PER_TILE, PACK], F32)

        w_raw = [keep.tile([P, PACK, D], BF16, name="w_raw%d" % h) for h in range(2)]
        w_grouped = [keep.tile([P, D, PACK], BF16, name="w_grouped%d" % h, align_bytes=64) for h in range(2)]
        w_words = [keep.tile([P, D], U32, name="w_words%d" % h, align_bytes=64) for h in range(2)]
        w_scales = [keep.tile([P, D], U8, name="w_scales%d" % h, align_bytes=64) for h in range(2)]

        emb_col = keep.tile([P, PACK, D], BF16)
        c_stats = keep.tile([P, PACK, BN_STATS], F32)
        c_mean_var = keep.tile([P, PACK, BN_AGGR], F32)
        c_rstd = keep.tile([P, PACK], F32)
        c_mean_rstd = keep.tile([P, PACK], F32)
        c_shift = keep.tile([P, PACK], F32)
        c_norm = [keep.tile([P, D], F32, name="c_norm%d" % a) for a in range(PACK)]
        col_planes = keep.tile([P, PACK, D], BF16)
        col_grouped = keep.tile([P, D, PACK], BF16, align_bytes=64)
        col_words = keep.tile([P, D], U32, align_bytes=64)
        col_scales = keep.tile([P, D], U8, align_bytes=64)

        prev = [keep.tile([P, PAIR, D], BF16, name="prev%d" % c) for c in range(PAIRS)]
        prev_grouped = [
            keep.tile([P, PAIR * P * 2], F32, name="prev_grouped%d" % c, align_bytes=64) for c in range(PAIRS)
        ]
        prev_words = keep.tile([P, TILES * P], U32, align_bytes=64)
        prev_scales = keep.tile([P, TILES * P], U8, align_bytes=64)
        x_grouped = [keep.tile([P, PAIR, P, PACK], BF16, name="x_grouped%d" % c, align_bytes=64) for c in range(PAIRS)]
        x_words = keep.tile([P, TILES * P], U32, align_bytes=64)
        x_scales = keep.tile([P, TILES * P], U8, align_bytes=64)
        result = [keep.tile([P, PAIR, D], F32, name="result%d" % c) for c in range(PAIRS)]

        banks = {}
        steps = {}

        def step(name, engines, emit):
            steps[name] = (engines, emit)

        def copy_bits(engine, dst, src):
            if engine == VECTOR:
                nc.vector.tensor_copy(out=dst, in_=src)
            elif engine == SCALAR:
                nc.scalar.copy(out=dst, in_=src)
            else:
                nc.gpsimd.tensor_scalar(out=dst, in0=src, scalar1=1.0, scalar2=0.0, op0=ALU.mult, op1=ALU.add)

        def gain_and_bias(engine, dst, src, gain, bias):
            if engine == SCALAR:
                nc.scalar.activation(out=dst, in_=src, func=ACT.Identity, scale=gain, bias=bias)
            else:
                nc.vector.tensor_scalar(out=dst, in0=src, scalar1=gain, scalar2=bias, op0=ALU.mult, op1=ALU.add)

        def rstd(dst, variance):
            nc.scalar.activation(out=dst, in_=variance, func=ACT.Abs_reciprocal_sqrt, bias=eps[:])

        def vector_column(v, t):
            return vectors[:, PACK * v + t : PACK * v + t + 1]

        def regroup(engine, grouped, planes, cols):
            copy_bits(
                engine,
                grouped[:, cols, :].rearrange("p (c i) t -> p c t i", i=RUN),
                planes[:, :, cols].rearrange("p t (c i) -> p c t i", i=RUN),
            )

        def quantise(words, scales, values):
            nc.vector.quantize_mx(out=words.bitcast(FP8X4), scales=scales, in_=values)

        def matmul_mx(dst, l_words, l_scales, r_words, r_scales):
            nc.tensor.matmul_mx(
                out=dst,
                lhsT=l_words.bitcast(FP8X4),
                lhsT_scale=l_scales,
                rhs=r_words.bitcast(FP8X4),
                rhs_scale=r_scales,
                start=True,
                stop=True,
            )

        def span(i, width=P):
            return slice(i * width, (i + 1) * width)

        def clear(engine):
            nc.vector.memset(vector_rows[:], 0.0)
            nc.vector.memset(zero[:], 0.0)
            nc.vector.tensor_scalar_add(out=eps[:], in0=zero[:], scalar1=EPS)

        def load_vectors(engine):
            for v, vec in enumerate((ln_prompt_w, ln_prompt_b, b_imp, ln_col_w, ln_col_b)):
                nc.sync.dma_start(out=vector_rows[PACK * v : PACK * (v + 1), :], in_=vec.rearrange("(t c) -> t c", c=P))

        def load_w1(engine):
            nc.sync.dma_start(
                out=w_raw[1][:].rearrange("p (u e) c -> p u (e c)", u=2),
                in_=w_imp[D : 2 * D, :].rearrange("(u p e) c -> p u (e c)", u=2, e=2),
            )

        step("clear", (VECTOR,), clear)
        step("rstd_table", (SCALAR,), lambda engine: rstd(table_loaded[:], eps[:]))
        step("identity_f32", (GPSIMD,), lambda engine: make_identity(nc, identity_f32[:]))
        step("identity_bf16", (GPSIMD,), lambda engine: make_identity(nc, identity_bf16[:]))
        step("load_prompt", (SYNC,), lambda engine: nc.sync.dma_start(out=prompt[:], in_=emb_prompt))
        step("load_vectors", (SYNC,), load_vectors)
        for h in range(2):
            step(
                "load_column%d" % h,
                (SYNC,),
                lambda engine, h=h: nc.sync.dma_start(
                    out=emb_col[:, span(h, PACK // 2), :],
                    in_=emb_column.rearrange("(q a) d -> q a d", a=PACK)[:, span(h, PACK // 2), :],
                ),
            )
        step(
            "load_w0",
            (SYNC,),
            lambda engine: nc.sync.dma_start(out=w_raw[0][:], in_=w_imp[0:D, :].rearrange("(t p) c -> p t c", p=P)),
        )
        step("load_w1", (SYNC,), load_w1)
        for c in range(PAIRS):
            step(
                "load_prev%d" % c,
                (SYNC,),
                lambda engine, c=c: nc.sync.dma_start(out=prev[c][:], in_=prev_rows[:, span(c, PAIR), :]),
            )

        def t_vectors(engine):
            banks["vectors"] = ps_t.tile([P, P], BF16, tag="t", name="vectors_ps")
            nc.tensor.transpose(banks["vectors"][:], vector_rows[:], identity_bf16[:])

        step("T_vectors", (TENSOR,), t_vectors)
        step(
            "vectors",
            (SCALAR,),
            lambda engine: copy_bits(engine, vectors[:], banks["vectors"][:, 0 : N_VECTORS * PACK]),
        )

        def p_stats_step(engine):
            nc.vector.bn_stats(out=p_stats[:], in_=prompt[:])
            nc.vector.bn_aggr(out=p_mean_var[:], in_=p_stats[:])

        def t_p_norm(engine):
            banks["p_norm"] = ps_t.tile([P, PACK, P], F32, tag="t", name="p_norm_ps")
            for t in range(PACK):
                nc.tensor.transpose(banks["p_norm"][:, t, :], p_norm[:, span(t)], identity_f32[:])

        def p_gain(engine):
            for t in range(PACK):
                gain_and_bias(
                    engine,
                    pn_planes[:, t, :],
                    banks["p_norm"][:, t, :],
                    vector_column(LN_PROMPT_W, t),
                    vector_column(LN_PROMPT_B, t),
                )

        step("p_stats", (VECTOR,), p_stats_step)
        step("p_rstd", (SCALAR,), lambda engine: rstd(p_rstd[:], p_mean_var[:, 1:2]))
        step(
            "p_norm",
            (VECTOR,),
            lambda engine: nc.vector.tensor_scalar(
                out=p_norm[:],
                in0=prompt[:],
                scalar1=p_mean_var[:, 0:1],
                scalar2=p_rstd[:],
                op0=ALU.subtract,
                op1=ALU.mult,
            ),
        )
        step("T_p_norm", (TENSOR,), t_p_norm)
        step("p_gain", (SCALAR,), p_gain)
        step(
            "p_group",
            (VECTOR,),
            lambda engine: copy_bits(engine, pn_grouped[:], pn_planes[:].rearrange("p t r -> p r t")),
        )
        step(
            "p_quant",
            (VECTOR,),
            lambda engine: quantise(pn_words[:], pn_scales[:], pn_grouped[:].rearrange("p r t -> p (r t)")),
        )

        def t_prompt(engine):
            banks["prompt"] = ps_t.tile([P, PACK, P], BF16, tag="t", name="prompt_ps")
            for t in range(PACK):
                nc.tensor.transpose(banks["prompt"][:, t, :], prompt[:, span(t)], identity_bf16[:])

        def p_bias(engine):
            nc.vector.tensor_tensor(
                out=prompt_bias[:],
                in0=banks["prompt"][:],
                in1=vectors[:, span(B_IMP, PACK)].unsqueeze(2).to_broadcast([P, PACK, P]),
                op=ALU.add,
            )

        step("T_prompt", (TENSOR,), t_prompt)
        step("p_bias", (VECTOR,), p_bias)

        for h in range(2):
            for i in range(QUARTERS):
                step(
                    "w%d_group%d" % (h, i),
                    (VECTOR, SCALAR, GPSIMD),
                    lambda engine, h=h, i=i: regroup(engine, w_grouped[h], w_raw[h], span(i, D // QUARTERS)),
                )
            step(
                "w%d_quant" % h,
                (VECTOR,),
                lambda engine, h=h: quantise(
                    w_words[h][:], w_scales[h][:], w_grouped[h][:].rearrange("p c t -> p (c t)")
                ),
            )

        def mm_prompt(engine):
            banks["from_prompt"] = ps_x.tile([P, PACK, P], F32, tag="x", name="from_prompt_ps")
            for t in range(PACK):
                matmul_mx(
                    banks["from_prompt"][:, t, :],
                    w_words[0][:, span(t)],
                    w_scales[0][:, span(t)],
                    pn_words[:],
                    pn_scales[:],
                )

        def shared_step(engine):
            nc.vector.tensor_tensor(
                out=shared[:].rearrange("p j i t -> p i j t"),
                in0=banks["from_prompt"][:].rearrange("p t (i j) -> p i j t", j=TILES),
                in1=prompt_bias[:].rearrange("p t (i j) -> p i j t", j=TILES),
                op=ALU.add,
            )

        step("mm_prompt", (TENSOR,), mm_prompt)
        step("shared", (VECTOR,), shared_step)

        def c_stats_step(engine, a):
            nc.vector.bn_stats(out=c_stats[:, a, :], in_=emb_col[:, a, :])

        def c_aggr_step(engine, a):
            nc.vector.bn_aggr(out=c_mean_var[:, a, :], in_=c_stats[:, a, :])

        def c_shift_step(engine):
            nc.gpsimd.tensor_tensor(out=c_mean_rstd[:], in0=c_mean_var[:, :, 0], in1=c_rstd[:], op=ALU.mult)
            nc.gpsimd.tensor_scalar(
                out=c_shift[:], in0=c_mean_rstd[:], scalar1=-1.0, scalar2=0.0, op0=ALU.mult, op1=ALU.add
            )

        def c_norm_step(engine, a):
            one_col = slice(a, a + 1)
            if engine == SCALAR:
                nc.scalar.activation(
                    out=c_norm[a][:],
                    in_=emb_col[:, a, :],
                    func=ACT.Identity,
                    scale=c_rstd[:, one_col],
                    bias=c_shift[:, one_col],
                )
            else:
                nc.gpsimd.tensor_scalar(
                    out=c_norm[a][:],
                    in0=emb_col[:, a, :],
                    scalar1=c_rstd[:, one_col],
                    scalar2=c_shift[:, one_col],
                    op0=ALU.mult,
                    op1=ALU.add,
                )

        def t_c_norm(engine, t):
            banks["c_norm%d" % t] = ps_o.tile([P, PACK, P], F32, tag="o", name="c_norm_ps%d" % t)
            for a in range(PACK):
                nc.tensor.transpose(banks["c_norm%d" % t][:, a, :], c_norm[a][:, span(t)], identity_f32[:])

        def c_gain(engine, t):
            gain_and_bias(
                engine,
                col_planes[:, t, :].rearrange("p (q a) -> p q a", a=PACK),
                banks["c_norm%d" % t][:].rearrange("p a q -> p q a"),
                vector_column(LN_COL_W, t),
                vector_column(LN_COL_B, t),
            )

        for a in range(PACK):
            step("c_stats%d" % a, (VECTOR,), lambda engine, a=a: c_stats_step(engine, a))
            step("c_aggr%d" % a, (VECTOR,), lambda engine, a=a: c_aggr_step(engine, a))
            step("c_norm%d" % a, (SCALAR, GPSIMD), lambda engine, a=a: c_norm_step(engine, a))
        for t in range(PACK):
            step("T_c_norm%d" % t, (TENSOR,), lambda engine, t=t: t_c_norm(engine, t))
            step("c_gain%d" % t, (SCALAR, VECTOR), lambda engine, t=t: c_gain(engine, t))
        step("c_rstd", (SCALAR,), lambda engine: rstd(c_rstd[:], c_mean_var[:, :, 1]))
        step("c_shift", (GPSIMD,), c_shift_step)
        for h in range(HALVES):
            step(
                "c_group%d" % h,
                (SCALAR, GPSIMD),
                lambda engine, h=h: regroup(engine, col_grouped, col_planes, span(h, HALF)),
            )
        step(
            "c_quant",
            (VECTOR,),
            lambda engine: quantise(col_words[:], col_scales[:], col_grouped[:].rearrange("p c t -> p (c t)")),
        )

        def t_prev(engine, c):
            words = prev[c][:].rearrange("p s d -> p (s d)").bitcast(F32)
            banks["prev%d" % c] = ps_t.tile([P, PAIR, 2, P], F32, tag="t", name="prev_ps%d" % c)
            for s in range(PAIR):
                for u in range(2):
                    nc.tensor.transpose(banks["prev%d" % c][:, s, u, :], words[:, span(2 * s + u)], identity_f32[:])

        def prev_copy(engine, c):
            copy_bits(
                engine,
                prev_grouped[c][:].rearrange("p (s r u) -> p s r u", s=PAIR, u=2),
                banks["prev%d" % c][:].rearrange("p s u r -> p s r u"),
            )

        def mm_x(engine, j):
            banks["x%d" % j] = ps_x.tile([P, PACK, P], F32, tag="x", name="x_ps%d" % j)
            for t in range(PACK):
                matmul_mx(
                    banks["x%d" % j][:, t, :],
                    w_words[1][:, span(t)],
                    w_scales[1][:, span(t)],
                    prev_words[:, span(j)],
                    prev_scales[:, span(j)],
                )

        def x_add(engine, j):
            nc.vector.tensor_tensor(
                out=x_grouped[j // PAIR][:, j % PAIR].rearrange("p (m i) t -> p m i t", i=PER_TILE),
                in0=banks["x%d" % j][:].rearrange("p t (m i) -> p m i t", i=PER_TILE),
                in1=shared[:, j].unsqueeze(1).to_broadcast([P, P // PER_TILE, PER_TILE, PACK]),
                op=ALU.add,
            )

        def mm_out(engine, j):
            banks["out%d" % j] = ps_o.tile([P, D], F32, tag="o", name="out_ps%d" % j)
            matmul_mx(banks["out%d" % j][:], x_words[:, span(j)], x_scales[:, span(j)], col_words[:], col_scales[:])

        for c in range(PAIRS):
            step("T_prev%d" % c, (TENSOR,), lambda engine, c=c: t_prev(engine, c))
            step("prev_copy%d" % c, (SCALAR, VECTOR), lambda engine, c=c: prev_copy(engine, c))
            step(
                "prev_quant%d" % c,
                (VECTOR,),
                lambda engine, c=c: quantise(
                    prev_words[:, span(c, PAIR * P)],
                    prev_scales[:, span(c, PAIR * P)],
                    prev_grouped[c][:].bitcast(BF16),
                ),
            )
        for j in range(TILES):
            step("mm_x%d" % j, (TENSOR,), lambda engine, j=j: mm_x(engine, j))
            step("x_add%d" % j, (VECTOR,), lambda engine, j=j: x_add(engine, j))
            step("mm_out%d" % j, (TENSOR,), lambda engine, j=j: mm_out(engine, j))
            step(
                "out_copy%d" % j,
                (SCALAR, VECTOR),
                lambda engine, j=j: copy_bits(engine, result[j // PAIR][:, j % PAIR, :], banks["out%d" % j][:]),
            )
        for c in range(PAIRS - 1):
            step(
                "x_quant%d" % c,
                (VECTOR,),
                lambda engine, c=c: quantise(
                    x_words[:, span(c, PAIR * P)],
                    x_scales[:, span(c, PAIR * P)],
                    x_grouped[c][:].rearrange("p s r t -> p (s r t)"),
                ),
            )
        for c in range(TILE_STORES // PAIR):
            step(
                "store%d" % c,
                (SYNC,),
                lambda engine, c=c: nc.sync.dma_start(out=out_rows[:, span(c, PAIR), :], in_=result[c][:]),
            )
        for j in range(TILES - PAIR, TILES):
            step(
                "x_quant_tile%d" % j,
                (VECTOR,),
                lambda engine, j=j: quantise(
                    x_words[:, span(j)],
                    x_scales[:, span(j)],
                    x_grouped[j // PAIR][:, j % PAIR].rearrange("p r t -> p (r t)"),
                ),
            )
        for j in range(TILE_STORES, TILES):
            step(
                "store_tile%d" % j,
                (SYNC,),
                lambda engine, j=j: nc.sync.dma_start(out=out_rows[:, j, :], in_=result[j // PAIR][:, j % PAIR, :]),
            )

        assert sorted([name for row in SCHEDULE for name in row if name]) == sorted(steps)
        for row in SCHEDULE:
            for engine, name in zip(ENGINES, row):
                if name:
                    engines, emit = steps[name]
                    assert engine in engines, name
                    emit(engine)
